import numpy as np
import ml_dtypes


def mxq(x, axis, fmt="e4m3"):
    dtype, down = {"e4m3": (ml_dtypes.float8_e4m3fn, 7), "e5m2": (ml_dtypes.float8_e5m2, 14)}[fmt]
    v = np.moveaxis(np.asarray(x, np.float32).astype(ml_dtypes.bfloat16).astype(np.float64), axis, -1)
    blocks = v.reshape(v.shape[:-1] + (-1, 32))
    amax = np.abs(blocks).max(-1, keepdims=True)
    byte = np.maximum(np.where(amax > 0, np.frexp(amax)[1] - 1 + 127, 0) - down, 1)
    scale = np.exp2(byte - 127.0)
    codes = (blocks / scale).astype(np.float32).astype(dtype).astype(np.float64)
    return np.moveaxis((codes * scale).reshape(v.shape), -1, axis)


WIDE = False


def mx_kscale(k):
    if not WIDE:
        return np.ones(k)
    levels = np.array([10, -10, 5, -5, 0])
    if k % 512:
        return np.exp2(np.random.permutation(np.resize(levels, k // 32))).repeat(32)
    a = np.empty((k // 512, 16))
    for p in range(k // 512):
        a[p, :8] = np.random.permutation(np.resize(levels, 8))
        for g in range(8):
            far = levels[np.abs(levels - a[p, g]) >= 10]
            a[p, g + 8] = far[np.random.randint(len(far))]
    return np.exp2(a.ravel()).repeat(32)


BF16 = ml_dtypes.bfloat16


def bf(x):
    return np.asarray(x, np.float32).astype(BF16)


def f64(x):
    return np.asarray(x).astype(np.float64)


B, S, K, C_IN, H, HO = 8, 112, 16, 768, 2048, 2048
N = S + K
BN_EPS = 1e-5


def group_bn(z, g, b):
    m = z.mean(axis=1, keepdims=True)
    v = z.var(axis=1, keepdims=True)
    return (z - m) * (1.0 / np.sqrt(v + BN_EPS)) * g + b


def setup_inputs():
    t = mx_kscale(H)
    sd = 2.0 * np.exp2(-12.0 * np.random.random((B, 1, H)))
    z1 = sd * (np.random.standard_normal((B, N, H)) + 0.5 * np.random.standard_normal((B, 1, H)))
    return {"z1": bf(z1),
            "g1": bf((1.0 + 0.3 * np.random.standard_normal(H)) * t),
            "be1": bf(0.3 * np.random.standard_normal(H) * t),
            "W2": bf(np.random.standard_normal((H, HO)) / np.sqrt(H) / t[:, None]),
            "b2": bf(np.random.standard_normal(HO))}


def reference(z1, g1, be1, W2, b2):
    h = np.maximum(group_bn(f64(z1), f64(g1), f64(be1)), 0.0)
    return (mxq(h, 2, "e4m3") @ mxq(f64(W2), 0, "e4m3")) + f64(b2)

@@ -1,0 +1,306 @@
+from contextlib import ExitStack
+
+import concourse.mybir as mybir
+from concourse.masks import make_identity
+
+FP8X4 = mybir.dt.float8_e4m3fn_x4
+BF16 = mybir.dt.bfloat16
+F32 = mybir.dt.float32
+U32 = mybir.dt.uint32
+U8 = mybir.dt.uint8
+ACT = mybir.ActivationFunctionType
+ALU = mybir.AluOpType
+
+P = 128
+PACK = 4
+GROUPS = 8
+H = 2048
+HO = 2048
+K_PASSES = H // (P * PACK)
+CHUNKS = H // P
+N_TILE = 512
+N_BLOCKS = HO // N_TILE
+BN_EPS = 1e-5
+
+PAIRS = 2 * GROUPS
+PAIR_CHUNKS = 2 * PACK
+W_OPERANDS = N_BLOCKS * K_PASSES
+W_AHEAD = 2
+ACC_BANKS = 4
+
+FLOPS = 2 * GROUPS * P * H * HO
+
+
+def interleave(nc, grouped, planes):
+    nc.vector.tensor_copy(
+        out=grouped.rearrange("p (m i) t -> p m t i", i=4),
+        in_=planes.rearrange("p t (m i) -> p m t i", i=4),
+    )
+
+
+def tile_vocohead_pa_kernel(tc, z1, g1, be1, W2, b2, out):
+    nc = tc.nc
+    with ExitStack() as ctx:
+        const = ctx.enter_context(tc.tile_pool(name="const", bufs=1))
+        inputs = ctx.enter_context(tc.tile_pool(name="inputs", bufs=1))
+        keep = ctx.enter_context(tc.tile_pool(name="keep", bufs=1))
+        stage = ctx.enter_context(tc.tile_pool(name="stage", bufs=3))
+        stats = ctx.enter_context(tc.tile_pool(name="stats", bufs=4))
+        results = ctx.enter_context(tc.tile_pool(name="results", bufs=6))
+        centred_pool = ctx.enter_context(tc.psum_pool(name="centred", bufs=4))
+        acc_pool = ctx.enter_context(tc.psum_pool(name="acc", bufs=ACC_BANKS))
+
+        vector_rows = const.tile([P, P], BF16)
+        nc.vector.memset(vector_rows[64:128, :], 0.0)
+        for i in range(4):
+            nc.scalar.dma_start(
+                out=vector_rows[i * CHUNKS : (i + 1) * CHUNKS, :],
+                in_=b2.rearrange("(a p) -> a p", p=P),
+            )
+        pass_rows = const.tile([P, PACK * P], BF16)
+        nc.gpsimd.memset(pass_rows[:], 0.0)
+        for i, vector in enumerate((g1, be1)):
+            nc.scalar.dma_start(
+                out=pass_rows[i * K_PASSES : (i + 1) * K_PASSES, :],
+                in_=vector.rearrange("(c f) -> c f", c=K_PASSES),
+            )
+        z_sb = []
+        w_raw = []
+
+        def load_weights(k):
+            nb, c = divmod(k, K_PASSES)
+            w_tile = inputs.tile([P, PACK, N_TILE], BF16, name="w%d" % k)
+            nc.sync.dma_start(
+                out=w_tile[:],
+                in_=W2[
+                    c * PACK * P : (c + 1) * PACK * P, nb * N_TILE : (nb + 1) * N_TILE
+                ].rearrange("(p t) n -> p t n", t=PACK),
+            )
+            w_raw.append(w_tile)
+
+        for b in range(GROUPS):
+            load_weights(2 * b)
+            z_tile = inputs.tile([P, H], BF16, name="z%d" % b)
+            nc.sync.dma_start(out=z_tile[:], in_=z1[b])
+            z_sb.append(z_tile)
+            load_weights(2 * b + 1)
+
+        ident = const.tile([P, P], BF16)
+        make_identity(nc, ident[:])
+        centre_matrix = const.tile([P, P], BF16)
+        nc.vector.tensor_scalar_add(out=centre_matrix[:], in0=ident[:], scalar1=-1.0 / P)
+        one = const.tile([P, 1], F32)
+        nc.vector.memset(one[:], 1.0)
+        warm = const.tile([P, 1], F32)
+        nc.scalar.activation(out=warm[:], in_=one[:], func=ACT.Sqrt)
+
+        columns_ps = centred_pool.tile([P, P], BF16, tag="centred")
+        nc.tensor.transpose(out=columns_ps[:], in_=vector_rows[:], identity=ident[:])
+        features_ps = centred_pool.tile([P, PACK, P], BF16, tag="centred")
+        for t in range(PACK):
+            nc.tensor.transpose(
+                out=features_ps[:, t, :], in_=pass_rows[:, t : PACK * P : PACK], identity=ident[:]
+            )
+        gain0 = const.tile([P, CHUNKS], F32)
+        nc.vector.tensor_scalar_mul(
+            out=gain0[:].rearrange("p (c t) -> p t c", t=PACK),
+            in0=features_ps[:, :, 0:K_PASSES],
+            scalar1=BN_EPS**-0.5,
+        )
+        shift = const.tile([P, CHUNKS], F32)
+        nc.vector.tensor_copy(
+            out=shift[:].rearrange("p (c t) -> p t c", t=PACK),
+            in_=features_ps[:, :, K_PASSES : 2 * K_PASSES],
+        )
+        b2_columns = const.tile([P, CHUNKS], BF16)
+        nc.vector.tensor_copy(out=b2_columns[:], in_=columns_ps[:, 0:CHUNKS])
+
+        w_codes = keep.tile([P, W_OPERANDS, N_TILE], U32, align_bytes=64)
+        w_scales = keep.tile([P, W_OPERANDS, N_TILE], U8, align_bytes=64)
+        h_codes = keep.tile([P, PAIRS, 2 * P], U32, align_bytes=64)
+        h_scales = keep.tile([P, PAIRS, 2 * P], U8, align_bytes=64)
+
+        banks = {}
+        sumsq = {}
+        spread = {}
+        inverse = {}
+        gain = {}
+        planes = {}
+        h_grouped = {}
+        w_grouped = {}
+
+        def centre(pair, j):
+            b, first = pair // 2, (pair % 2) * PAIR_CHUNKS + j * PACK
+            bank = centred_pool.tile([P, PACK, P], F32, tag="centred")
+            for t in range(PACK):
+                a = first + t
+                nc.tensor.matmul(
+                    out=bank[:, t, :],
+                    lhsT=z_sb[b][:, (a // PACK) * PACK * P + a % PACK : (a // PACK + 1) * PACK * P : PACK],
+                    rhs=centre_matrix[:],
+                    start=True,
+                    stop=True,
+                )
+            banks[(pair, j)] = bank
+
+        def squares(pair):
+            sumsq[pair] = stats.tile([P, PAIR_CHUNKS], F32, name="sumsq")
+            unread = stage.tile([P, PAIR_CHUNKS, P], BF16, name="unread")
+            for i in range(PAIR_CHUNKS):
+                nc.scalar.activation(
+                    out=unread[:, i, :],
+                    in_=banks[(pair, i // PACK)][:, i % PACK, :],
+                    func=ACT.Square,
+                    accum_out=sumsq[pair][:, i : i + 1],
+                )
+
+        def root(pair):
+            spread[pair] = stats.tile([P, PAIR_CHUNKS], F32, name="spread")
+            nc.scalar.activation(
+                out=spread[pair][:],
+                in_=sumsq[pair][:],
+                func=ACT.Sqrt,
+                bias=one[:, 0:1],
+                scale=1.0 / (P * BN_EPS),
+            )
+
+        def invert(pair):
+            inverse[pair] = stats.tile([P, PAIR_CHUNKS], F32, name="inverse")
+            nc.vector.reciprocal(out=inverse[pair][:], in_=spread[pair][:])
+
+        def scale_gain(pair):
+            first = (pair % 2) * PAIR_CHUNKS
+            gain[pair] = stats.tile([P, PAIR_CHUNKS], F32, name="gain")
+            nc.vector.tensor_mul(
+                out=gain[pair][:], in0=inverse[pair][:], in1=gain0[:, first : first + PAIR_CHUNKS]
+            )
+
+        def normalise(pair, j):
+            if j == 0:
+                planes[pair] = stage.tile([P, PACK, 2, P], BF16, name="planes")
+            for t in range(PACK):
+                i = j * PACK + t
+                a = (pair % 2) * PAIR_CHUNKS + i
+                nc.scalar.activation(
+                    out=planes[pair][:, t, j, :],
+                    in_=banks[(pair, j)][:, t, :],
+                    func=ACT.Relu,
+                    bias=shift[:, a : a + 1],
+                    scale=gain[pair][:, i : i + 1],
+                )
+
+        def interleave_h(pair):
+            h_grouped[pair] = stage.tile([P, 2, P, PACK], BF16, align_bytes=64, name="h_grouped")
+            nc.scalar.copy(
+                out=h_grouped[pair][:, 0, :, :].rearrange("p (m i) t -> p m t i", i=4),
+                in_=planes[pair][:, :, 0, :].rearrange("p t (m i) -> p m t i", i=4),
+            )
+            interleave(nc, h_grouped[pair][:, 1, :, :], planes[pair][:, :, 1, :])
+
+        def quantise_h(pair):
+            nc.vector.quantize_mx(
+                out=h_codes[:, pair, :].bitcast(FP8X4),
+                scales=h_scales[:, pair, :],
+                in_=h_grouped[pair][:].rearrange("p j r t -> p (j r t)"),
+            )
+
+        def interleave_w(k):
+            w_grouped[k] = stage.tile([P, N_TILE, PACK], BF16, align_bytes=64, name="w_grouped")
+            interleave(nc, w_grouped[k][:], w_raw[k][:])
+
+        def quantise_w(k):
+            nc.vector.quantize_mx(
+                out=w_codes[:, k, :].bitcast(FP8X4),
+                scales=w_scales[:, k, :],
+                in_=w_grouped[k][:].rearrange("p n t -> p (n t)"),
+            )
+
+        def multiply(b, nb):
+            acc = acc_pool.tile([P, N_TILE], F32, name="acc")
+            for c in range(K_PASSES):
+                rows = slice((c % 2) * P, (c % 2 + 1) * P)
+                nc.tensor.matmul_mx(
+                    out=acc[:],
+                    lhsT=h_codes[:, 2 * b + c // 2, rows].bitcast(FP8X4),
+                    lhsT_scale=h_scales[:, 2 * b + c // 2, rows],
+                    rhs=w_codes[:, K_PASSES * nb + c, :].bitcast(FP8X4),
+                    rhs_scale=w_scales[:, K_PASSES * nb + c, :],
+                    start=(c == 0),
+                    stop=(c == K_PASSES - 1),
+                )
+            return acc
+
+        def add_bias_and_store(acc, b, nb):
+            cols = slice(nb * N_TILE, (nb + 1) * N_TILE)
+            result = results.tile([P, N_TILE], F32, name="result")
+            nc.vector.tensor_tensor(out=result[:], in0=acc[:], in1=b2_all[:, cols], op=ALU.add)
+            nc.sync.dma_start(out=out[b, :, cols], in_=result[:])
+
+        for pair in (0, 1):
+            centre(pair, 0)
+            centre(pair, 1)
+        for k in range(W_AHEAD):
+            interleave_w(k)
+        for k in range(W_AHEAD):
+            quantise_w(k)
+        squares(0)
+        root(0)
+        invert(0)
+        scale_gain(0)
+
+        b2_all = const.tile([P, HO], BF16)
+        for nb in range(N_BLOCKS):
+            b2_ps = acc_pool.tile([P, PACK, P], F32, name="acc")
+            for t in range(PACK):
+                a = PACK * nb + t
+                nc.tensor.matmul(
+                    out=b2_ps[:, t, :],
+                    lhsT=b2_columns[:, a : a + 1].to_broadcast([P, P]),
+                    rhs=ident[:],
+                    start=True,
+                    stop=True,
+                )
+            nc.vector.tensor_copy(
+                out=b2_all[:, nb * N_TILE : (nb + 1) * N_TILE],
+                in_=b2_ps[:].rearrange("p t n -> p (t n)"),
+            )
+
+        multiplied = set()
+        in_psum = []
+        slot = 0
+        while len(multiplied) < GROUPS * N_BLOCKS or in_psum:
+            if slot + 1 < PAIRS:
+                squares(slot + 1)
+            for j in range(2):
+                if slot < PAIRS:
+                    normalise(slot, j)
+                if slot + 2 < PAIRS:
+                    centre(slot + 2, j)
+                if j == 0 and slot + 1 < PAIRS:
+                    root(slot + 1)
+
+            k = slot + W_AHEAD
+            if slot + 1 < PAIRS:
+                invert(slot + 1)
+            if 1 <= slot <= PAIRS:
+                interleave_h(slot - 1)
+            if slot + 1 < PAIRS:
+                scale_gain(slot + 1)
+            if k < W_OPERANDS:
+                interleave_w(k)
+            if 1 <= slot <= PAIRS:
+                quantise_h(slot - 1)
+            for acc, b, nb in in_psum:
+                add_bias_and_store(acc, b, nb)
+            in_psum = []
+            if k < W_OPERANDS:
+                quantise_w(k)
+
+            groups_ready = min(slot // 2, GROUPS)
+            blocks_ready = min(k + 1, W_OPERANDS) // K_PASSES
+            for b in range(groups_ready):
+                for nb in range(blocks_ready):
+                    if (b, nb) not in multiplied and len(in_psum) < ACC_BANKS:
+                        multiplied.add((b, nb))
+                        in_psum.append((multiply(b, nb), b, nb))
+            slot += 1

@@ -25,8 +25,9 @@ BN_EPS = 1e-5
 PAIRS = 2 * GROUPS
 PAIR_CHUNKS = 2 * PACK
 W_OPERANDS = N_BLOCKS * K_PASSES
-W_AHEAD = 2
+W_AHEAD = 4
 ACC_BANKS = 4
+B2_AFTER = 2
 
 FLOPS = 2 * GROUPS * P * H * HO
 
@@ -50,20 +51,17 @@ def tile_vocohead_pa_kernel(tc, z1, g1, be1, W2, b2, out):
         centred_pool = ctx.enter_context(tc.psum_pool(name="centred", bufs=4))
         acc_pool = ctx.enter_context(tc.psum_pool(name="acc", bufs=ACC_BANKS))
 
-        vector_rows = const.tile([P, P], BF16)
-        nc.vector.memset(vector_rows[64:128, :], 0.0)
-        for i in range(4):
-            nc.scalar.dma_start(
-                out=vector_rows[i * CHUNKS : (i + 1) * CHUNKS, :],
-                in_=b2.rearrange("(a p) -> a p", p=P),
-            )
         pass_rows = const.tile([P, PACK * P], BF16)
-        nc.gpsimd.memset(pass_rows[:], 0.0)
         for i, vector in enumerate((g1, be1)):
             nc.scalar.dma_start(
                 out=pass_rows[i * K_PASSES : (i + 1) * K_PASSES, :],
                 in_=vector.rearrange("(c f) -> c f", c=K_PASSES),
             )
+        nc.scalar.dma_start(out=pass_rows[8:16, :], in_=z1[0, 0:8, 0 : PACK * P])
+        nc.scalar.dma_start(out=pass_rows[16:32, :], in_=z1[0, 0:16, 0 : PACK * P])
+        nc.gpsimd.memset(pass_rows[32:64, :], 0.0)
+        nc.gpsimd.memset(pass_rows[64:128, :], 0.0)
+        b2_all = const.tile([P, HO], BF16)
         z_sb = []
         w_raw = []
 
@@ -79,11 +77,18 @@ def tile_vocohead_pa_kernel(tc, z1, g1, be1, W2, b2, out):
             w_raw.append(w_tile)
 
         for b in range(GROUPS):
-            load_weights(2 * b)
             z_tile = inputs.tile([P, H], BF16, name="z%d" % b)
-            nc.sync.dma_start(out=z_tile[:], in_=z1[b])
             z_sb.append(z_tile)
+            if b == 0:
+                for half in range(2):
+                    cols = slice(half * H // 2, (half + 1) * H // 2)
+                    nc.sync.dma_start(out=z_tile[:, cols], in_=z1[b, :, cols])
+            load_weights(2 * b)
+            if b > 0:
+                nc.sync.dma_start(out=z_tile[:], in_=z1[b])
             load_weights(2 * b + 1)
+            if b == B2_AFTER:
+                nc.sync.dma_start(out=b2_all[:], in_=b2.partition_broadcast(P))
 
         ident = const.tile([P, P], BF16)
         make_identity(nc, ident[:])
@@ -92,28 +97,7 @@ def tile_vocohead_pa_kernel(tc, z1, g1, be1, W2, b2, out):
         one = const.tile([P, 1], F32)
         nc.vector.memset(one[:], 1.0)
         warm = const.tile([P, 1], F32)
-        nc.scalar.activation(out=warm[:], in_=one[:], func=ACT.Sqrt)
-
-        columns_ps = centred_pool.tile([P, P], BF16, tag="centred")
-        nc.tensor.transpose(out=columns_ps[:], in_=vector_rows[:], identity=ident[:])
-        features_ps = centred_pool.tile([P, PACK, P], BF16, tag="centred")
-        for t in range(PACK):
-            nc.tensor.transpose(
-                out=features_ps[:, t, :], in_=pass_rows[:, t : PACK * P : PACK], identity=ident[:]
-            )
-        gain0 = const.tile([P, CHUNKS], F32)
-        nc.vector.tensor_scalar_mul(
-            out=gain0[:].rearrange("p (c t) -> p t c", t=PACK),
-            in0=features_ps[:, :, 0:K_PASSES],
-            scalar1=BN_EPS**-0.5,
-        )
-        shift = const.tile([P, CHUNKS], F32)
-        nc.vector.tensor_copy(
-            out=shift[:].rearrange("p (c t) -> p t c", t=PACK),
-            in_=features_ps[:, :, K_PASSES : 2 * K_PASSES],
-        )
-        b2_columns = const.tile([P, CHUNKS], BF16)
-        nc.vector.tensor_copy(out=b2_columns[:], in_=columns_ps[:, 0:CHUNKS])
+        nc.scalar.activation(out=warm[:], in_=one[:], func=ACT.Abs_reciprocal_sqrt)
 
         w_codes = keep.tile([P, W_OPERANDS, N_TILE], U32, align_bytes=64)
         w_scales = keep.tile([P, W_OPERANDS, N_TILE], U8, align_bytes=64)
@@ -122,7 +106,6 @@ def tile_vocohead_pa_kernel(tc, z1, g1, be1, W2, b2, out):
 
         banks = {}
         sumsq = {}
-        spread = {}
         inverse = {}
         gain = {}
         planes = {}
@@ -155,24 +138,23 @@ def tile_vocohead_pa_kernel(tc, z1, g1, be1, W2, b2, out):
                 )
 
         def root(pair):
-            spread[pair] = stats.tile([P, PAIR_CHUNKS], F32, name="spread")
+            inverse[pair] = stats.tile([P, PAIR_CHUNKS], F32, name="inverse")
             nc.scalar.activation(
-                out=spread[pair][:],
+                out=inverse[pair][:],
                 in_=sumsq[pair][:],
-                func=ACT.Sqrt,
+                func=ACT.Abs_reciprocal_sqrt,
                 bias=one[:, 0:1],
                 scale=1.0 / (P * BN_EPS),
             )
 
-        def invert(pair):
-            inverse[pair] = stats.tile([P, PAIR_CHUNKS], F32, name="inverse")
-            nc.vector.reciprocal(out=inverse[pair][:], in_=spread[pair][:])
-
         def scale_gain(pair):
             first = (pair % 2) * PAIR_CHUNKS
             gain[pair] = stats.tile([P, PAIR_CHUNKS], F32, name="gain")
-            nc.vector.tensor_mul(
-                out=gain[pair][:], in0=inverse[pair][:], in1=gain0[:, first : first + PAIR_CHUNKS]
+            nc.gpsimd.tensor_tensor(
+                out=gain[pair][:],
+                in0=inverse[pair][:],
+                in1=gain0[:, first : first + PAIR_CHUNKS],
+                op=ALU.mult,
             )
 
         def normalise(pair, j):
@@ -215,9 +197,10 @@ def tile_vocohead_pa_kernel(tc, z1, g1, be1, W2, b2, out):
                 in_=w_grouped[k][:].rearrange("p n t -> p (n t)"),
             )
 
-        def multiply(b, nb):
-            acc = acc_pool.tile([P, N_TILE], F32, name="acc")
-            for c in range(K_PASSES):
+        def multiply(b, nb, acc=None, passes=range(K_PASSES)):
+            if acc is None:
+                acc = acc_pool.tile([P, N_TILE], F32, name="acc")
+            for c in passes:
                 rows = slice((c % 2) * P, (c % 2 + 1) * P)
                 nc.tensor.matmul_mx(
                     out=acc[:],
@@ -239,32 +222,34 @@ def tile_vocohead_pa_kernel(tc, z1, g1, be1, W2, b2, out):
         for pair in (0, 1):
             centre(pair, 0)
             centre(pair, 1)
-        for k in range(W_AHEAD):
-            interleave_w(k)
-        for k in range(W_AHEAD):
-            quantise_w(k)
+        features_ps = acc_pool.tile([P, PACK, P], BF16, name="acc")
+        for t in range(PACK):
+            nc.tensor.transpose(
+                out=features_ps[:, t, :], in_=pass_rows[:, t : PACK * P : PACK], identity=ident[:]
+            )
+        gain0 = const.tile([P, CHUNKS], F32)
+        nc.vector.tensor_scalar_mul(
+            out=gain0[:].rearrange("p (c t) -> p t c", t=PACK),
+            in0=features_ps[:, :, 0:K_PASSES],
+            scalar1=BN_EPS**-0.5,
+        )
+        shift = const.tile([P, CHUNKS], F32)
+        nc.vector.tensor_copy(
+            out=shift[:].rearrange("p (c t) -> p t c", t=PACK),
+            in_=features_ps[:, :, K_PASSES : 2 * K_PASSES],
+        )
+
         squares(0)
         root(0)
-        invert(0)
         scale_gain(0)
+        for k in range(W_AHEAD):
+            interleave_w(k)
+            if k >= 1:
+                quantise_w(k - 1)
+        quantise_w(W_AHEAD - 1)
 
-        b2_all = const.tile([P, HO], BF16)
-        for nb in range(N_BLOCKS):
-            b2_ps = acc_pool.tile([P, PACK, P], F32, name="acc")
-            for t in range(PACK):
-                a = PACK * nb + t
-                nc.tensor.matmul(
-                    out=b2_ps[:, t, :],
-                    lhsT=b2_columns[:, a : a + 1].to_broadcast([P, P]),
-                    rhs=ident[:],
-                    start=True,
-                    stop=True,
-                )
-            nc.vector.tensor_copy(
-                out=b2_all[:, nb * N_TILE : (nb + 1) * N_TILE],
-                in_=b2_ps[:].rearrange("p t n -> p (t n)"),
-            )
-
+        LAST = GROUPS - 1
+        last_acc = []
         multiplied = set()
         in_psum = []
         slot = 0
@@ -278,14 +263,11 @@ def tile_vocohead_pa_kernel(tc, z1, g1, be1, W2, b2, out):
                     centre(slot + 2, j)
                 if j == 0 and slot + 1 < PAIRS:
                     root(slot + 1)
+                    scale_gain(slot + 1)
 
             k = slot + W_AHEAD
-            if slot + 1 < PAIRS:
-                invert(slot + 1)
             if 1 <= slot <= PAIRS:
                 interleave_h(slot - 1)
-            if slot + 1 < PAIRS:
-                scale_gain(slot + 1)
             if k < W_OPERANDS:
                 interleave_w(k)
             if 1 <= slot <= PAIRS:
@@ -296,11 +278,18 @@ def tile_vocohead_pa_kernel(tc, z1, g1, be1, W2, b2, out):
             if k < W_OPERANDS:
                 quantise_w(k)
 
-            groups_ready = min(slot // 2, GROUPS)
+            groups_ready = min(slot // 2, LAST)
             blocks_ready = min(k + 1, W_OPERANDS) // K_PASSES
             for b in range(groups_ready):
                 for nb in range(blocks_ready):
                     if (b, nb) not in multiplied and len(in_psum) < ACC_BANKS:
                         multiplied.add((b, nb))
                         in_psum.append((multiply(b, nb), b, nb))
+            if slot == PAIRS - 1:
+                assert not in_psum and len(multiplied) == LAST * N_BLOCKS
+                last_acc = [multiply(LAST, nb, None, (0, 1)) for nb in range(N_BLOCKS)]
+            if slot == PAIRS:
+                for nb in range(N_BLOCKS):
+                    multiplied.add((LAST, nb))
+                    in_psum.append((multiply(LAST, nb, last_acc[nb], (2, 3)), LAST, nb))
             slot += 1

@@ -150,11 +150,8 @@ def tile_vocohead_pa_kernel(tc, z1, g1, be1, W2, b2, out):
         def scale_gain(pair):
             first = (pair % 2) * PAIR_CHUNKS
             gain[pair] = stats.tile([P, PAIR_CHUNKS], F32, name="gain")
-            nc.gpsimd.tensor_tensor(
-                out=gain[pair][:],
-                in0=inverse[pair][:],
-                in1=gain0[:, first : first + PAIR_CHUNKS],
-                op=ALU.mult,
+            nc.vector.tensor_mul(
+                out=gain[pair][:], in0=inverse[pair][:], in1=gain0[:, first : first + PAIR_CHUNKS]
             )
 
         def normalise(pair, j):

@@ -27,7 +27,6 @@ PAIR_CHUNKS = 2 * PACK
 W_OPERANDS = N_BLOCKS * K_PASSES
 W_AHEAD = 4
 ACC_BANKS = 4
-B2_AFTER = 2
 
 FLOPS = 2 * GROUPS * P * H * HO
 
@@ -57,7 +56,8 @@ def tile_vocohead_pa_kernel(tc, z1, g1, be1, W2, b2, out):
                 out=pass_rows[i * K_PASSES : (i + 1) * K_PASSES, :],
                 in_=vector.rearrange("(c f) -> c f", c=K_PASSES),
             )
-        nc.scalar.dma_start(out=pass_rows[8:16, :], in_=z1[0, 0:8, 0 : PACK * P])
+        nc.scalar.dma_start(out=pass_rows[8:12, :], in_=b2.rearrange("(c f) -> c f", c=K_PASSES))
+        nc.scalar.dma_start(out=pass_rows[12:16, :], in_=b2.rearrange("(c f) -> c f", c=K_PASSES))
         nc.scalar.dma_start(out=pass_rows[16:32, :], in_=z1[0, 0:16, 0 : PACK * P])
         nc.gpsimd.memset(pass_rows[32:64, :], 0.0)
         nc.gpsimd.memset(pass_rows[64:128, :], 0.0)
@@ -87,8 +87,6 @@ def tile_vocohead_pa_kernel(tc, z1, g1, be1, W2, b2, out):
             if b > 0:
                 nc.sync.dma_start(out=z_tile[:], in_=z1[b])
             load_weights(2 * b + 1)
-            if b == B2_AFTER:
-                nc.sync.dma_start(out=b2_all[:], in_=b2.partition_broadcast(P))
 
         ident = const.tile([P, P], BF16)
         make_identity(nc, ident[:])
@@ -239,6 +237,25 @@ def tile_vocohead_pa_kernel(tc, z1, g1, be1, W2, b2, out):
         squares(0)
         root(0)
         scale_gain(0)
+        b2_columns = const.tile([P, PACK, K_PASSES], BF16)
+        nc.vector.tensor_copy(out=b2_columns[:], in_=features_ps[:, :, 2 * K_PASSES : 3 * K_PASSES])
+        for half in range(2):
+            b2_ps = acc_pool.tile([P, 2, PACK, P], BF16, name="acc")
+            for i in range(2):
+                for t in range(PACK):
+                    nc.tensor.matmul(
+                        out=b2_ps[:, i, t, :],
+                        lhsT=b2_columns[:, t, 2 * half + i : 2 * half + i + 1].to_broadcast([P, P]),
+                        rhs=ident[:],
+                        start=True,
+                        stop=True,
+                    )
+            nc.vector.tensor_copy(
+                out=b2_all[:, half * 2 * N_TILE : (half + 1) * 2 * N_TILE].rearrange(
+                    "p (i n t) -> p i n t", i=2, t=PACK
+                ),
+                in_=b2_ps[:].rearrange("p i t n -> p i n t"),
+            )
         for k in range(W_AHEAD):
             interleave_w(k)
             if k >= 1:

@@ -27,6 +27,7 @@ PAIR_CHUNKS = 2 * PACK
 W_OPERANDS = N_BLOCKS * K_PASSES
 W_AHEAD = 4
 ACC_BANKS = 4
+S_WORDS = 64
 
 FLOPS = 2 * GROUPS * P * H * HO
 
@@ -52,13 +53,13 @@ def tile_vocohead_pa_kernel(tc, z1, g1, be1, W2, b2, out):
 
         pass_rows = const.tile([P, PACK * P], BF16)
         for i, vector in enumerate((g1, be1)):
-            nc.scalar.dma_start(
+            nc.sync.dma_start(
                 out=pass_rows[i * K_PASSES : (i + 1) * K_PASSES, :],
                 in_=vector.rearrange("(c f) -> c f", c=K_PASSES),
             )
-        nc.scalar.dma_start(out=pass_rows[8:12, :], in_=b2.rearrange("(c f) -> c f", c=K_PASSES))
-        nc.scalar.dma_start(out=pass_rows[12:16, :], in_=b2.rearrange("(c f) -> c f", c=K_PASSES))
-        nc.scalar.dma_start(out=pass_rows[16:32, :], in_=z1[0, 0:16, 0 : PACK * P])
+        nc.sync.dma_start(out=pass_rows[8:12, :], in_=b2.rearrange("(c f) -> c f", c=K_PASSES))
+        nc.sync.dma_start(out=pass_rows[12:16, :], in_=b2.rearrange("(c f) -> c f", c=K_PASSES))
+        nc.sync.dma_start(out=pass_rows[16:32, :], in_=z1[0, 0:16, 0 : PACK * P])
         nc.gpsimd.memset(pass_rows[32:64, :], 0.0)
         nc.gpsimd.memset(pass_rows[64:128, :], 0.0)
         b2_all = const.tile([P, HO], BF16)
@@ -168,11 +169,13 @@ def tile_vocohead_pa_kernel(tc, z1, g1, be1, W2, b2, out):
 
         def interleave_h(pair):
             h_grouped[pair] = stage.tile([P, 2, P, PACK], BF16, align_bytes=64, name="h_grouped")
+            words = h_grouped[pair][:].rearrange("p j r t -> p (j r) t")
+            rows = planes[pair][:].rearrange("p t j r -> p t (j r)")
             nc.scalar.copy(
-                out=h_grouped[pair][:, 0, :, :].rearrange("p (m i) t -> p m t i", i=4),
-                in_=planes[pair][:, :, 0, :].rearrange("p t (m i) -> p m t i", i=4),
+                out=words[:, 0:S_WORDS, :].rearrange("p (m i) t -> p m t i", i=4),
+                in_=rows[:, :, 0:S_WORDS].rearrange("p t (m i) -> p m t i", i=4),
             )
-            interleave(nc, h_grouped[pair][:, 1, :, :], planes[pair][:, :, 1, :])
+            interleave(nc, words[:, S_WORDS:, :], rows[:, :, S_WORDS:])
 
         def quantise_h(pair):
             nc.vector.quantize_mx(

@@ -27,7 +27,7 @@ PAIR_CHUNKS = 2 * PACK
 W_OPERANDS = N_BLOCKS * K_PASSES
 W_AHEAD = 4
 ACC_BANKS = 4
-S_WORDS = 64
+S_WORDS = 128
 
 FLOPS = 2 * GROUPS * P * H * HO
 
@@ -50,53 +50,6 @@ def tile_vocohead_pa_kernel(tc, z1, g1, be1, W2, b2, out):
         results = ctx.enter_context(tc.tile_pool(name="results", bufs=6))
         centred_pool = ctx.enter_context(tc.psum_pool(name="centred", bufs=4))
         acc_pool = ctx.enter_context(tc.psum_pool(name="acc", bufs=ACC_BANKS))
-
-        pass_rows = const.tile([P, PACK * P], BF16)
-        for i, vector in enumerate((g1, be1)):
-            nc.sync.dma_start(
-                out=pass_rows[i * K_PASSES : (i + 1) * K_PASSES, :],
-                in_=vector.rearrange("(c f) -> c f", c=K_PASSES),
-            )
-        nc.sync.dma_start(out=pass_rows[8:12, :], in_=b2.rearrange("(c f) -> c f", c=K_PASSES))
-        nc.sync.dma_start(out=pass_rows[12:16, :], in_=b2.rearrange("(c f) -> c f", c=K_PASSES))
-        nc.sync.dma_start(out=pass_rows[16:32, :], in_=z1[0, 0:16, 0 : PACK * P])
-        nc.gpsimd.memset(pass_rows[32:64, :], 0.0)
-        nc.gpsimd.memset(pass_rows[64:128, :], 0.0)
-        b2_all = const.tile([P, HO], BF16)
-        z_sb = []
-        w_raw = []
-
-        def load_weights(k):
-            nb, c = divmod(k, K_PASSES)
-            w_tile = inputs.tile([P, PACK, N_TILE], BF16, name="w%d" % k)
-            nc.sync.dma_start(
-                out=w_tile[:],
-                in_=W2[
-                    c * PACK * P : (c + 1) * PACK * P, nb * N_TILE : (nb + 1) * N_TILE
-                ].rearrange("(p t) n -> p t n", t=PACK),
-            )
-            w_raw.append(w_tile)
-
-        for b in range(GROUPS):
-            z_tile = inputs.tile([P, H], BF16, name="z%d" % b)
-            z_sb.append(z_tile)
-            if b == 0:
-                for half in range(2):
-                    cols = slice(half * H // 2, (half + 1) * H // 2)
-                    nc.sync.dma_start(out=z_tile[:, cols], in_=z1[b, :, cols])
-            load_weights(2 * b)
-            if b > 0:
-                nc.sync.dma_start(out=z_tile[:], in_=z1[b])
-            load_weights(2 * b + 1)
-
-        ident = const.tile([P, P], BF16)
-        make_identity(nc, ident[:])
-        centre_matrix = const.tile([P, P], BF16)
-        nc.vector.tensor_scalar_add(out=centre_matrix[:], in0=ident[:], scalar1=-1.0 / P)
-        one = const.tile([P, 1], F32)
-        nc.vector.memset(one[:], 1.0)
-        warm = const.tile([P, 1], F32)
-        nc.scalar.activation(out=warm[:], in_=one[:], func=ACT.Abs_reciprocal_sqrt)
 
         w_codes = keep.tile([P, W_OPERANDS, N_TILE], U32, align_bytes=64)
         w_scales = keep.tile([P, W_OPERANDS, N_TILE], U8, align_bytes=64)
@@ -217,53 +170,115 @@ def tile_vocohead_pa_kernel(tc, z1, g1, be1, W2, b2, out):
             nc.vector.tensor_tensor(out=result[:], in0=acc[:], in1=b2_all[:, cols], op=ALU.add)
             nc.sync.dma_start(out=out[b, :, cols], in_=result[:])
 
-        for pair in (0, 1):
-            centre(pair, 0)
-            centre(pair, 1)
-        features_ps = acc_pool.tile([P, PACK, P], BF16, name="acc")
-        for t in range(PACK):
-            nc.tensor.transpose(
-                out=features_ps[:, t, :], in_=pass_rows[:, t : PACK * P : PACK], identity=ident[:]
-            )
-        gain0 = const.tile([P, CHUNKS], F32)
-        nc.vector.tensor_scalar_mul(
-            out=gain0[:].rearrange("p (c t) -> p t c", t=PACK),
-            in0=features_ps[:, :, 0:K_PASSES],
-            scalar1=BN_EPS**-0.5,
-        )
-        shift = const.tile([P, CHUNKS], F32)
-        nc.vector.tensor_copy(
-            out=shift[:].rearrange("p (c t) -> p t c", t=PACK),
-            in_=features_ps[:, :, K_PASSES : 2 * K_PASSES],
-        )
+        with tc.manual_schedule():
+            pass_rows = const.tile([P, PACK * P], BF16)
+            b2_all = const.tile([P, HO], BF16)
+            z_sb = []
+            w_raw = []
 
-        squares(0)
-        root(0)
-        scale_gain(0)
-        b2_columns = const.tile([P, PACK, K_PASSES], BF16)
-        nc.vector.tensor_copy(out=b2_columns[:], in_=features_ps[:, :, 2 * K_PASSES : 3 * K_PASSES])
-        for half in range(2):
-            b2_ps = acc_pool.tile([P, 2, PACK, P], BF16, name="acc")
-            for i in range(2):
-                for t in range(PACK):
-                    nc.tensor.matmul(
-                        out=b2_ps[:, i, t, :],
-                        lhsT=b2_columns[:, t, 2 * half + i : 2 * half + i + 1].to_broadcast([P, P]),
-                        rhs=ident[:],
-                        start=True,
-                        stop=True,
-                    )
-            nc.vector.tensor_copy(
-                out=b2_all[:, half * 2 * N_TILE : (half + 1) * 2 * N_TILE].rearrange(
-                    "p (i n t) -> p i n t", i=2, t=PACK
-                ),
-                in_=b2_ps[:].rearrange("p i t n -> p i n t"),
+            def load_weights(k):
+                nb, c = divmod(k, K_PASSES)
+                w_tile = inputs.tile([P, PACK, N_TILE], BF16, name="w%d" % k)
+                nc.sync.dma_start(
+                    out=w_tile[:],
+                    in_=W2[
+                        c * PACK * P : (c + 1) * PACK * P, nb * N_TILE : (nb + 1) * N_TILE
+                    ].rearrange("(p t) n -> p t n", t=PACK),
+                )
+                w_raw.append(w_tile)
+
+            def load_group(b, first, last):
+                cols = slice(first * PACK * P, last * PACK * P)
+                nc.sync.dma_start(out=z_sb[b][:, cols], in_=z1[b, :, cols])
+
+            for b in range(GROUPS):
+                z_tile = inputs.tile([P, H], BF16, name="z%d" % b)
+                z_sb.append(z_tile)
+            load_weights(0)
+            load_group(0, 0, 2)
+            load_weights(1)
+            for i, vector in enumerate((g1, be1, b2, b2)):
+                nc.sync.dma_start(
+                    out=pass_rows[i * K_PASSES : (i + 1) * K_PASSES, :],
+                    in_=vector.rearrange("(c f) -> c f", c=K_PASSES),
+                )
+            nc.sync.dma_start(out=pass_rows[16:32, :], in_=z1[0, 0:16, 0 : PACK * P])
+            load_group(0, 2, 4)
+            for b in range(1, GROUPS):
+                load_weights(2 * b)
+                load_group(b, 0, 4)
+                load_weights(2 * b + 1)
+
+            ident = const.tile([P, P], BF16)
+            make_identity(nc, ident[:])
+            nc.gpsimd.memset(pass_rows[32:64, :], 0.0)
+            nc.gpsimd.memset(pass_rows[64:128, :], 0.0)
+            centre_matrix = const.tile([P, P], BF16)
+            nc.vector.tensor_scalar_add(out=centre_matrix[:], in0=ident[:], scalar1=-1.0 / P)
+            one = const.tile([P, 1], F32)
+            nc.vector.memset(one[:], 1.0)
+            warm = const.tile([P, 1], F32)
+            nc.scalar.activation(out=warm[:], in_=one[:], func=ACT.Abs_reciprocal_sqrt)
+
+            def spread_b2(half):
+                nc.vector.tensor_copy(
+                    out=b2_all[:, half * 2 * N_TILE : (half + 1) * 2 * N_TILE].rearrange(
+                        "p (i n t) -> p i n t", i=2, t=PACK
+                    ),
+                    in_=b2_banks[half][:].rearrange("p i t n -> p i n t"),
+                )
+
+            interleave_w(0)
+            centre(0, 0)
+            centre(0, 1)
+            squares(0)
+            root(0)
+            quantise_w(0)
+            interleave_w(1)
+            features_ps = acc_pool.tile([P, PACK, P], BF16, name="acc")
+            for t in range(PACK):
+                nc.tensor.transpose(
+                    out=features_ps[:, t, :], in_=pass_rows[:, t : PACK * P : PACK], identity=ident[:]
+                )
+            centre(1, 0)
+            centre(1, 1)
+            squares(1)
+            root(1)
+            gain0 = const.tile([P, CHUNKS], F32)
+            nc.vector.tensor_scalar_mul(
+                out=gain0[:].rearrange("p (c t) -> p t c", t=PACK),
+                in0=features_ps[:, :, 0:K_PASSES],
+                scalar1=BN_EPS**-0.5,
             )
-        for k in range(W_AHEAD):
-            interleave_w(k)
-            if k >= 1:
-                quantise_w(k - 1)
-        quantise_w(W_AHEAD - 1)
+            shift = const.tile([P, CHUNKS], F32)
+            nc.vector.tensor_copy(
+                out=shift[:].rearrange("p (c t) -> p t c", t=PACK),
+                in_=features_ps[:, :, K_PASSES : 2 * K_PASSES],
+            )
+            scale_gain(0)
+            b2_columns = const.tile([P, PACK, K_PASSES], BF16)
+            nc.vector.tensor_copy(out=b2_columns[:], in_=features_ps[:, :, 2 * K_PASSES : 3 * K_PASSES])
+            b2_banks = []
+            for half in range(2):
+                b2_ps = acc_pool.tile([P, 2, PACK, P], BF16, name="acc")
+                for i in range(2):
+                    for t in range(PACK):
+                        nc.tensor.matmul(
+                            out=b2_ps[:, i, t, :],
+                            lhsT=b2_columns[:, t, 2 * half + i : 2 * half + i + 1].to_broadcast([P, P]),
+                            rhs=ident[:],
+                            start=True,
+                            stop=True,
+                        )
+                b2_banks.append(b2_ps)
+            quantise_w(1)
+            scale_gain(1)
+            interleave_w(2)
+            spread_b2(0)
+            quantise_w(2)
+            interleave_w(3)
+            spread_b2(1)
+            quantise_w(3)
 
         LAST = GROUPS - 1
         last_acc = []
@@ -271,14 +286,14 @@ def tile_vocohead_pa_kernel(tc, z1, g1, be1, W2, b2, out):
         in_psum = []
         slot = 0
         while len(multiplied) < GROUPS * N_BLOCKS or in_psum:
-            if slot + 1 < PAIRS:
+            if 1 <= slot < PAIRS - 1:
                 squares(slot + 1)
             for j in range(2):
                 if slot < PAIRS:
                     normalise(slot, j)
                 if slot + 2 < PAIRS:
                     centre(slot + 2, j)
-                if j == 0 and slot + 1 < PAIRS:
+                if j == 0 and 1 <= slot < PAIRS - 1:
                     root(slot + 1)
                     scale_gain(slot + 1)
 

@@ -27,6 +27,7 @@ PAIR_CHUNKS = 2 * PACK
 W_OPERANDS = N_BLOCKS * K_PASSES
 W_AHEAD = 4
 ACC_BANKS = 4
+RUN = 8
 S_WORDS = 128
 
 FLOPS = 2 * GROUPS * P * H * HO
@@ -34,8 +35,8 @@ FLOPS = 2 * GROUPS * P * H * HO
 
 def interleave(nc, grouped, planes):
     nc.vector.tensor_copy(
-        out=grouped.rearrange("p (m i) t -> p m t i", i=4),
-        in_=planes.rearrange("p t (m i) -> p m t i", i=4),
+        out=grouped.rearrange("p (m i) t -> p m t i", i=RUN),
+        in_=planes.rearrange("p t (m i) -> p m t i", i=RUN),
     )
 
 
@@ -125,8 +126,8 @@ def tile_vocohead_pa_kernel(tc, z1, g1, be1, W2, b2, out):
             words = h_grouped[pair][:].rearrange("p j r t -> p (j r) t")
             rows = planes[pair][:].rearrange("p t j r -> p t (j r)")
             nc.scalar.copy(
-                out=words[:, 0:S_WORDS, :].rearrange("p (m i) t -> p m t i", i=4),
-                in_=rows[:, :, 0:S_WORDS].rearrange("p t (m i) -> p m t i", i=4),
+                out=words[:, 0:S_WORDS, :].rearrange("p (m i) t -> p m t i", i=RUN),
+                in_=rows[:, :, 0:S_WORDS].rearrange("p t (m i) -> p m t i", i=RUN),
             )
             interleave(nc, words[:, S_WORDS:, :], rows[:, :, S_WORDS:])
 
@@ -222,10 +223,8 @@ def tile_vocohead_pa_kernel(tc, z1, g1, be1, W2, b2, out):
 
             def spread_b2(half):
                 nc.vector.tensor_copy(
-                    out=b2_all[:, half * 2 * N_TILE : (half + 1) * 2 * N_TILE].rearrange(
-                        "p (i n t) -> p i n t", i=2, t=PACK
-                    ),
-                    in_=b2_banks[half][:].rearrange("p i t n -> p i n t"),
+                    out=b2_all[:, half * 2 * N_TILE : (half + 1) * 2 * N_TILE],
+                    in_=b2_banks[half][:].rearrange("p a n -> p (a n)"),
                 )
 
             interleave_w(0)
@@ -235,10 +234,14 @@ def tile_vocohead_pa_kernel(tc, z1, g1, be1, W2, b2, out):
             root(0)
             quantise_w(0)
             interleave_w(1)
-            features_ps = acc_pool.tile([P, PACK, P], BF16, name="acc")
+            features_ps = acc_pool.tile([P, 2 * PACK, P], BF16, name="acc")
             for t in range(PACK):
                 nc.tensor.transpose(
                     out=features_ps[:, t, :], in_=pass_rows[:, t : PACK * P : PACK], identity=ident[:]
+                )
+            for s in range(PACK):
+                nc.tensor.transpose(
+                    out=features_ps[:, PACK + s, :], in_=pass_rows[:, s * P : (s + 1) * P], identity=ident[:]
                 )
             centre(1, 0)
             centre(1, 1)
@@ -247,29 +250,31 @@ def tile_vocohead_pa_kernel(tc, z1, g1, be1, W2, b2, out):
             gain0 = const.tile([P, CHUNKS], F32)
             nc.vector.tensor_scalar_mul(
                 out=gain0[:].rearrange("p (c t) -> p t c", t=PACK),
-                in0=features_ps[:, :, 0:K_PASSES],
+                in0=features_ps[:, 0:PACK, 0:K_PASSES],
                 scalar1=BN_EPS**-0.5,
             )
             shift = const.tile([P, CHUNKS], F32)
             nc.vector.tensor_copy(
                 out=shift[:].rearrange("p (c t) -> p t c", t=PACK),
-                in_=features_ps[:, :, K_PASSES : 2 * K_PASSES],
+                in_=features_ps[:, 0:PACK, K_PASSES : 2 * K_PASSES],
             )
             scale_gain(0)
             b2_columns = const.tile([P, PACK, K_PASSES], BF16)
-            nc.vector.tensor_copy(out=b2_columns[:], in_=features_ps[:, :, 2 * K_PASSES : 3 * K_PASSES])
+            nc.vector.tensor_copy(
+                out=b2_columns[:], in_=features_ps[:, PACK : 2 * PACK, 2 * K_PASSES : 3 * K_PASSES]
+            )
             b2_banks = []
             for half in range(2):
-                b2_ps = acc_pool.tile([P, 2, PACK, P], BF16, name="acc")
-                for i in range(2):
-                    for t in range(PACK):
-                        nc.tensor.matmul(
-                            out=b2_ps[:, i, t, :],
-                            lhsT=b2_columns[:, t, 2 * half + i : 2 * half + i + 1].to_broadcast([P, P]),
-                            rhs=ident[:],
-                            start=True,
-                            stop=True,
-                        )
+                b2_ps = acc_pool.tile([P, 2 * PACK, P], BF16, name="acc")
+                for i in range(2 * PACK):
+                    c, s = divmod(2 * PACK * half + i, PACK)
+                    nc.tensor.matmul(
+                        out=b2_ps[:, i, :],
+                        lhsT=b2_columns[:, s, c : c + 1].to_broadcast([P, P]),
+                        rhs=ident[:],
+                        start=True,
+                        stop=True,
+                    )
                 b2_banks.append(b2_ps)
             quantise_w(1)
             scale_gain(1)

@@ -277,8 +277,8 @@ def tile_vocohead_pa_kernel(tc, z1, g1, be1, W2, b2, out):
                     )
                 b2_banks.append(b2_ps)
             quantise_w(1)
-            scale_gain(1)
             interleave_w(2)
+            scale_gain(1)
             spread_b2(0)
             quantise_w(2)
             interleave_w(3)

@@ -21,16 +21,36 @@ CHUNKS = H // P
 N_TILE = 512
 N_BLOCKS = HO // N_TILE
 BN_EPS = 1e-5
-
 PAIRS = 2 * GROUPS
 PAIR_CHUNKS = 2 * PACK
-W_OPERANDS = N_BLOCKS * K_PASSES
-W_AHEAD = 4
 ACC_BANKS = 4
 RUN = 8
 S_WORDS = 128
+MERGE_H = 0
+DBL = 4
+ROOT_EARLY = 1
+TAIL = 0
+B2S = 0
+HEADW = 4
+EARLY = 0
+ORDER = "FDdBEAC"
+PINV = 0
+SMODE = 0
+S_LATE = 128
+LATE_FROM = 99
+MXORD = 0
+ROOTP = 1
+HEADSQ = 1
+HLAG = 0
+WSCHED = None
 
 FLOPS = 2 * GROUPS * P * H * HO
+
+UNITS = [
+    (i * N_TILE, w * N_TILE, c_pass)
+    for (i, w) in [(i, 1) for i in range(DBL)] + [(i, 2) for i in range(DBL, N_BLOCKS, 2)]
+    for c_pass in range(K_PASSES)
+]
 
 
 def interleave(nc, grouped, planes):
@@ -48,14 +68,14 @@ def tile_vocohead_pa_kernel(tc, z1, g1, be1, W2, b2, out):
         keep = ctx.enter_context(tc.tile_pool(name="keep", bufs=1))
         stage = ctx.enter_context(tc.tile_pool(name="stage", bufs=3))
         stats = ctx.enter_context(tc.tile_pool(name="stats", bufs=4))
-        results = ctx.enter_context(tc.tile_pool(name="results", bufs=6))
+        results = ctx.enter_context(tc.tile_pool(name="results", bufs=20))
         centred_pool = ctx.enter_context(tc.psum_pool(name="centred", bufs=4))
         acc_pool = ctx.enter_context(tc.psum_pool(name="acc", bufs=ACC_BANKS))
 
-        w_codes = keep.tile([P, W_OPERANDS, N_TILE], U32, align_bytes=64)
-        w_scales = keep.tile([P, W_OPERANDS, N_TILE], U8, align_bytes=64)
-        h_codes = keep.tile([P, PAIRS, 2 * P], U32, align_bytes=64)
-        h_scales = keep.tile([P, PAIRS, 2 * P], U8, align_bytes=64)
+        w_codes = keep.tile([P, K_PASSES, HO], U32, align_bytes=64)
+        w_scales = keep.tile([P, K_PASSES, HO], U8, align_bytes=64)
+        h_codes = keep.tile([P, GROUPS, K_PASSES * P], U32, align_bytes=64)
+        h_scales = keep.tile([P, GROUPS, K_PASSES * P], U8, align_bytes=64)
 
         banks = {}
         sumsq = {}
@@ -79,12 +99,13 @@ def tile_vocohead_pa_kernel(tc, z1, g1, be1, W2, b2, out):
                 )
             banks[(pair, j)] = bank
 
-        def squares(pair):
-            sumsq[pair] = stats.tile([P, PAIR_CHUNKS], F32, name="sumsq")
-            unread = stage.tile([P, PAIR_CHUNKS, P], BF16, name="unread")
-            for i in range(PAIR_CHUNKS):
+        def squares(pair, j):
+            if j == 0:
+                sumsq[pair] = stats.tile([P, PAIR_CHUNKS], F32, name="sumsq")
+            unread = stage.tile([P, PACK, P], BF16, name="unread")
+            for i in range(j * PACK, (j + 1) * PACK):
                 nc.scalar.activation(
-                    out=unread[:, i, :],
+                    out=unread[:, i % PACK, :],
                     in_=banks[(pair, i // PACK)][:, i % PACK, :],
                     func=ACT.Square,
                     accum_out=sumsq[pair][:, i : i + 1],
@@ -107,14 +128,26 @@ def tile_vocohead_pa_kernel(tc, z1, g1, be1, W2, b2, out):
                 out=gain[pair][:], in0=inverse[pair][:], in1=gain0[:, first : first + PAIR_CHUNKS]
             )
 
+        def whole(b):
+            return b < MERGE_H
+
         def normalise(pair, j):
+            b = pair // 2
             if j == 0:
-                planes[pair] = stage.tile([P, PACK, 2, P], BF16, name="planes")
+                if whole(b):
+                    if pair % 2 == 0:
+                        g_planes = stage.tile([P, PACK, K_PASSES, P], BF16, name="g_planes")
+                        planes[pair] = g_planes
+                        planes[pair + 1] = g_planes
+                else:
+                    p_planes = stage.tile([P, PACK, 2, P], BF16, name="p_planes")
+                    planes[pair] = p_planes
+            slot_in = (2 * (pair % 2) if whole(b) else 0) + j
             for t in range(PACK):
                 i = j * PACK + t
                 a = (pair % 2) * PAIR_CHUNKS + i
                 nc.scalar.activation(
-                    out=planes[pair][:, t, j, :],
+                    out=planes[pair][:, t, slot_in, :],
                     in_=banks[(pair, j)][:, t, :],
                     func=ACT.Relu,
                     bias=shift[:, a : a + 1],
@@ -122,54 +155,86 @@ def tile_vocohead_pa_kernel(tc, z1, g1, be1, W2, b2, out):
                 )
 
         def interleave_h(pair):
-            h_grouped[pair] = stage.tile([P, 2, P, PACK], BF16, align_bytes=64, name="h_grouped")
-            words = h_grouped[pair][:].rearrange("p j r t -> p (j r) t")
+            if whole(pair // 2):
+                grouped = stage.tile([P, K_PASSES * P, PACK], BF16, align_bytes=64, name="g_grouped")
+                s_words = 2 * S_WORDS
+            else:
+                grouped = stage.tile([P, 2 * P, PACK], BF16, align_bytes=64, name="p_grouped")
+                s_words = S_LATE if pair >= LATE_FROM else S_WORDS
+            h_grouped[pair] = grouped
+            words = grouped[:]
             rows = planes[pair][:].rearrange("p t j r -> p t (j r)")
-            nc.scalar.copy(
-                out=words[:, 0:S_WORDS, :].rearrange("p (m i) t -> p m t i", i=RUN),
-                in_=rows[:, :, 0:S_WORDS].rearrange("p t (m i) -> p m t i", i=RUN),
-            )
-            interleave(nc, words[:, S_WORDS:, :], rows[:, :, S_WORDS:])
+            if s_words:
+                nc.scalar.copy(
+                    out=words[:, 0:s_words, :].rearrange("p (m i) t -> p m t i", i=RUN),
+                    in_=rows[:, :, 0:s_words].rearrange("p t (m i) -> p m t i", i=RUN),
+                )
+            interleave(nc, words[:, s_words:, :], rows[:, :, s_words:])
 
         def quantise_h(pair):
+            b = pair // 2
+            cols = slice(0, K_PASSES * P) if whole(b) else slice((pair % 2) * 2 * P, (pair % 2 + 1) * 2 * P)
             nc.vector.quantize_mx(
-                out=h_codes[:, pair, :].bitcast(FP8X4),
-                scales=h_scales[:, pair, :],
-                in_=h_grouped[pair][:].rearrange("p j r t -> p (j r t)"),
+                out=h_codes[:, b, cols].bitcast(FP8X4),
+                scales=h_scales[:, b, cols],
+                in_=h_grouped[pair][:].rearrange("p w t -> p (w t)"),
             )
 
-        def interleave_w(k):
-            w_grouped[k] = stage.tile([P, N_TILE, PACK], BF16, align_bytes=64, name="w_grouped")
-            interleave(nc, w_grouped[k][:], w_raw[k][:])
+        def interleave_w(u):
+            first, width, c = UNITS[u]
+            w_grp = stage.tile([P, width, PACK], BF16, align_bytes=64, name="w_grouped%d" % width)
+            w_grouped[u] = w_grp
+            interleave(nc, w_grp[:], w_raw[u][:])
 
-        def quantise_w(k):
+        def interleave_w_part(u, lo, hi, eng):
+            first, width, c = UNITS[u]
+            if u not in w_grouped:
+                w_grp = stage.tile([P, width, PACK], BF16, align_bytes=64, name="w_grouped%d" % width)
+                w_grouped[u] = w_grp
+            dst = w_grouped[u][:, lo:hi, :].rearrange("p (m i) t -> p m t i", i=RUN)
+            src = w_raw[u][:, :, lo:hi].rearrange("p t (m i) -> p m t i", i=RUN)
+            if eng == "S":
+                nc.scalar.copy(out=dst, in_=src)
+            else:
+                nc.vector.tensor_copy(out=dst, in_=src)
+
+        def quantise_w(u):
+            first, width, c = UNITS[u]
             nc.vector.quantize_mx(
-                out=w_codes[:, k, :].bitcast(FP8X4),
-                scales=w_scales[:, k, :],
-                in_=w_grouped[k][:].rearrange("p n t -> p (n t)"),
+                out=w_codes[:, c, first : first + width].bitcast(FP8X4),
+                scales=w_scales[:, c, first : first + width],
+                in_=w_grouped[u][:].rearrange("p n t -> p (n t)"),
             )
 
         def multiply(b, nb, acc=None, passes=range(K_PASSES)):
             if acc is None:
                 acc = acc_pool.tile([P, N_TILE], F32, name="acc")
+            n0 = nb * N_TILE
             for c in passes:
-                rows = slice((c % 2) * P, (c % 2 + 1) * P)
+                rows = slice(c * P, (c + 1) * P)
                 nc.tensor.matmul_mx(
                     out=acc[:],
-                    lhsT=h_codes[:, 2 * b + c // 2, rows].bitcast(FP8X4),
-                    lhsT_scale=h_scales[:, 2 * b + c // 2, rows],
-                    rhs=w_codes[:, K_PASSES * nb + c, :].bitcast(FP8X4),
-                    rhs_scale=w_scales[:, K_PASSES * nb + c, :],
+                    lhsT=h_codes[:, b, rows].bitcast(FP8X4),
+                    lhsT_scale=h_scales[:, b, rows],
+                    rhs=w_codes[:, c, n0 : n0 + N_TILE].bitcast(FP8X4),
+                    rhs_scale=w_scales[:, c, n0 : n0 + N_TILE],
                     start=(c == 0),
                     stop=(c == K_PASSES - 1),
                 )
             return acc
 
-        def add_bias_and_store(acc, b, nb):
-            cols = slice(nb * N_TILE, (nb + 1) * N_TILE)
+        def add_bias_and_store(acc, b, nb, pieces=1):
+            n0 = nb * N_TILE
             result = results.tile([P, N_TILE], F32, name="result")
-            nc.vector.tensor_tensor(out=result[:], in0=acc[:], in1=b2_all[:, cols], op=ALU.add)
-            nc.sync.dma_start(out=out[b, :, cols], in_=result[:])
+            w = N_TILE // pieces
+            for i in range(pieces):
+                nc.vector.tensor_tensor(
+                    out=result[:, i * w : (i + 1) * w],
+                    in0=acc[:, i * w : (i + 1) * w],
+                    in1=b2_all[:, n0 + i * w : n0 + (i + 1) * w],
+                    op=ALU.add,
+                )
+                nc.sync.dma_start(out=out[b, :, n0 + i * w : n0 + (i + 1) * w], in_=result[:, i * w : (i + 1) * w])
 
         with tc.manual_schedule():
             pass_rows = const.tile([P, PACK * P], BF16)
@@ -177,13 +242,13 @@ def tile_vocohead_pa_kernel(tc, z1, g1, be1, W2, b2, out):
             z_sb = []
             w_raw = []
 
-            def load_weights(k):
-                nb, c = divmod(k, K_PASSES)
-                w_tile = inputs.tile([P, PACK, N_TILE], BF16, name="w%d" % k)
+            def load_weights(u):
+                first, width, c = UNITS[u]
+                w_tile = inputs.tile([P, PACK, width], BF16, name="w%d" % u)
                 nc.sync.dma_start(
                     out=w_tile[:],
                     in_=W2[
-                        c * PACK * P : (c + 1) * PACK * P, nb * N_TILE : (nb + 1) * N_TILE
+                        c * PACK * P : (c + 1) * PACK * P, first : first + width
                     ].rearrange("(p t) n -> p t n", t=PACK),
                 )
                 w_raw.append(w_tile)
@@ -198,22 +263,30 @@ def tile_vocohead_pa_kernel(tc, z1, g1, be1, W2, b2, out):
             load_weights(0)
             load_group(0, 0, 2)
             load_weights(1)
-            for i, vector in enumerate((g1, be1, b2, b2)):
+            nc.vector.memset(pass_rows[:].bitcast(U32), 0)
+            for i, vector in enumerate((g1, be1, b2)):
                 nc.sync.dma_start(
                     out=pass_rows[i * K_PASSES : (i + 1) * K_PASSES, :],
                     in_=vector.rearrange("(c f) -> c f", c=K_PASSES),
                 )
-            nc.sync.dma_start(out=pass_rows[16:32, :], in_=z1[0, 0:16, 0 : PACK * P])
             load_group(0, 2, 4)
+            loaded = 2
+            total_cols = 0
             for b in range(1, GROUPS):
-                load_weights(2 * b)
+                want = b * 2 * N_TILE + N_TILE
+                while loaded < len(UNITS) and sum(UNITS[x][1] for x in range(loaded)) < want:
+                    load_weights(loaded)
+                    loaded += 1
                 load_group(b, 0, 4)
-                load_weights(2 * b + 1)
+                while loaded < len(UNITS) and sum(UNITS[x][1] for x in range(loaded)) < want + N_TILE:
+                    load_weights(loaded)
+                    loaded += 1
+            while loaded < len(UNITS):
+                load_weights(loaded)
+                loaded += 1
 
             ident = const.tile([P, P], BF16)
             make_identity(nc, ident[:])
-            nc.gpsimd.memset(pass_rows[32:64, :], 0.0)
-            nc.gpsimd.memset(pass_rows[64:128, :], 0.0)
             centre_matrix = const.tile([P, P], BF16)
             nc.vector.tensor_scalar_add(out=centre_matrix[:], in0=ident[:], scalar1=-1.0 / P)
             one = const.tile([P, 1], F32)
@@ -222,18 +295,21 @@ def tile_vocohead_pa_kernel(tc, z1, g1, be1, W2, b2, out):
             nc.scalar.activation(out=warm[:], in_=one[:], func=ACT.Abs_reciprocal_sqrt)
 
             def spread_b2(half):
-                nc.vector.tensor_copy(
-                    out=b2_all[:, half * 2 * N_TILE : (half + 1) * 2 * N_TILE],
-                    in_=b2_banks[half][:].rearrange("p a n -> p (a n)"),
-                )
+                src = b2_banks[half][:].rearrange("p a n -> p (a n)")
+                dst = b2_all[:, half * 2 * N_TILE : (half + 1) * 2 * N_TILE]
+                if B2S:
+                    nc.scalar.copy(out=dst, in_=src)
+                else:
+                    nc.vector.tensor_copy(out=dst, in_=src)
 
-            interleave_w(0)
+            interleave_w_part(0, 0, 512, "V")
             centre(0, 0)
             centre(0, 1)
-            squares(0)
+            squares(0, 0)
+            squares(0, 1)
             root(0)
             quantise_w(0)
-            interleave_w(1)
+            interleave_w_part(1, 0, 512, "V")
             features_ps = acc_pool.tile([P, 2 * PACK, P], BF16, name="acc")
             for t in range(PACK):
                 nc.tensor.transpose(
@@ -245,8 +321,10 @@ def tile_vocohead_pa_kernel(tc, z1, g1, be1, W2, b2, out):
                 )
             centre(1, 0)
             centre(1, 1)
-            squares(1)
-            root(1)
+            if HEADSQ:
+                squares(1, 0)
+                squares(1, 1)
+                root(1)
             gain0 = const.tile([P, CHUNKS], F32)
             nc.vector.tensor_scalar_mul(
                 out=gain0[:].rearrange("p (c t) -> p t c", t=PACK),
@@ -278,55 +356,117 @@ def tile_vocohead_pa_kernel(tc, z1, g1, be1, W2, b2, out):
                 b2_banks.append(b2_ps)
             quantise_w(1)
             interleave_w(2)
-            scale_gain(1)
-            spread_b2(0)
+            if HEADSQ:
+                scale_gain(1)
+            if not B2S:
+                spread_b2(0)
             quantise_w(2)
-            interleave_w(3)
-            spread_b2(1)
-            quantise_w(3)
+            if HEADW > 3:
+                interleave_w(3)
+            if not B2S:
+                spread_b2(1)
+            if HEADW > 3:
+                quantise_w(3)
 
         LAST = GROUPS - 1
         last_acc = []
+        half_acc = {}
         multiplied = set()
         in_psum = []
         slot = 0
+        w_done = HEADW
+        ready_cols = 0
+        sched = WSCHED if WSCHED is not None else [1] * 40
         while len(multiplied) < GROUPS * N_BLOCKS or in_psum:
-            if 1 <= slot < PAIRS - 1:
-                squares(slot + 1)
-            for j in range(2):
-                if slot < PAIRS:
-                    normalise(slot, j)
+            nxt = slot + 1 if (1 - HEADSQ) <= slot + 0 and slot + 1 < PAIRS and not (HEADSQ and slot == 0) else None
+            if slot < PAIRS:
+                if nxt is not None:
+                    squares(nxt, 0)
+                    if SMODE == 0:
+                        squares(nxt, 1)
+                        if ROOTP == 0:
+                            root(nxt)
+                normalise(slot, 0)
                 if slot + 2 < PAIRS:
-                    centre(slot + 2, j)
-                if j == 0 and 1 <= slot < PAIRS - 1:
-                    root(slot + 1)
-                    scale_gain(slot + 1)
-
-            k = slot + W_AHEAD
-            if 1 <= slot <= PAIRS:
-                interleave_h(slot - 1)
-            if k < W_OPERANDS:
-                interleave_w(k)
-            if 1 <= slot <= PAIRS:
-                quantise_h(slot - 1)
-            for acc, b, nb in in_psum:
-                add_bias_and_store(acc, b, nb)
+                    centre(slot + 2, 0)
+                if nxt is not None and SMODE == 0 and ROOTP == 1:
+                    root(nxt)
+                if nxt is not None and SMODE == 2:
+                    squares(nxt, 1)
+                    root(nxt)
+                normalise(slot, 1)
+                if slot + 2 < PAIRS:
+                    centre(slot + 2, 1)
+                if nxt is not None and SMODE == 1:
+                    squares(nxt, 1)
+                    root(nxt)
+            due = []
+            if 0 <= slot - HLAG < PAIRS:
+                pair = slot - HLAG
+                if not whole(pair // 2) or pair % 2 == 1:
+                    due = [pair]
+            units = []
+            n_units = sched[slot] if slot < len(sched) else 1
+            while n_units > 0 and w_done < len(UNITS):
+                units.append(w_done)
+                w_done += 1
+                n_units -= 1
+            def run_v(ch):
+                if ch == "A":
+                    for pair in due:
+                        interleave_h(pair)
+                elif ch == "B":
+                    for u in units:
+                        interleave_w(u)
+                elif ch == "C":
+                    for pair in due:
+                        quantise_h(pair)
+                elif ch == "D":
+                    for acc, b, nb in in_psum[: (len(in_psum) + 1) // 2]:
+                        add_bias_and_store(acc, b, nb)
+                elif ch == "d":
+                    for acc, b, nb in in_psum[(len(in_psum) + 1) // 2 :]:
+                        add_bias_and_store(acc, b, nb)
+                elif ch == "E":
+                    for u in units:
+                        quantise_w(u)
+                elif ch == "F":
+                    if nxt is not None:
+                        scale_gain(nxt)
+            if PINV:
+                with tc.manual_schedule(engines={mybir.EngineType.DVE}):
+                    for ch in ORDER:
+                        run_v(ch)
+            else:
+                for ch in ORDER:
+                    run_v(ch)
             in_psum = []
-            if k < W_OPERANDS:
-                quantise_w(k)
 
-            groups_ready = min(slot // 2, LAST)
-            blocks_ready = min(k + 1, W_OPERANDS) // K_PASSES
-            for b in range(groups_ready):
-                for nb in range(blocks_ready):
-                    if (b, nb) not in multiplied and len(in_psum) < ACC_BANKS:
+            pairs_done = slot + 1 - HLAG
+            groups_ready = min(pairs_done // 2, LAST)
+            cols_ready = [sum(1 for x in range(w_done) if UNITS[x][0] <= nb * N_TILE < UNITS[x][0] + UNITS[x][1]) == K_PASSES for nb in range(N_BLOCKS)]
+            cells = [(b, nb) for b in range(groups_ready) for nb in range(N_BLOCKS)]
+            if MXORD == 1:
+                cells.sort(key=lambda x: (x[1], x[0]))
+            if MXORD == 2:
+                cells.sort(key=lambda x: (-x[0], x[1]))
+            for b, nb in cells:
+                if True:
+                    if cols_ready[nb] and (b, nb) not in multiplied and len(in_psum) < ACC_BANKS:
                         multiplied.add((b, nb))
                         in_psum.append((multiply(b, nb), b, nb))
-            if slot == PAIRS - 1:
-                assert not in_psum and len(multiplied) == LAST * N_BLOCKS
-                last_acc = [multiply(LAST, nb, None, (0, 1)) for nb in range(N_BLOCKS)]
-            if slot == PAIRS:
-                for nb in range(N_BLOCKS):
-                    multiplied.add((LAST, nb))
-                    in_psum.append((multiply(LAST, nb, last_acc[nb], (2, 3)), LAST, nb))
+            if pairs_done == PAIRS - 1:
+                if not in_psum and len(multiplied) == LAST * N_BLOCKS:
+                    last_acc = [multiply(LAST, nb, None, (0, 1)) for nb in range(N_BLOCKS)]
+            if pairs_done >= PAIRS:
+                if last_acc:
+                    for nb in range(N_BLOCKS):
+                        if (LAST, nb) not in multiplied:
+                            multiplied.add((LAST, nb))
+                            in_psum.append((multiply(LAST, nb, last_acc[nb], (2, 3)), LAST, nb))
+                else:
+                    for nb in range(N_BLOCKS):
+                        if (LAST, nb) not in multiplied and len(in_psum) < ACC_BANKS:
+                            multiplied.add((LAST, nb))
+                            in_psum.append((multiply(LAST, nb), LAST, nb))
             slot += 1

@@ -21,36 +21,17 @@ CHUNKS = H // P
 N_TILE = 512
 N_BLOCKS = HO // N_TILE
 BN_EPS = 1e-5
+
 PAIRS = 2 * GROUPS
 PAIR_CHUNKS = 2 * PACK
+W_OPERANDS = N_BLOCKS * K_PASSES
+W_AHEAD = 4
 ACC_BANKS = 4
 RUN = 8
 S_WORDS = 128
-MERGE_H = 0
-DBL = 4
-ROOT_EARLY = 1
-TAIL = 0
-B2S = 0
-HEADW = 4
-EARLY = 0
-ORDER = "FDdBEAC"
-PINV = 0
-SMODE = 0
-S_LATE = 128
-LATE_FROM = 99
-MXORD = 0
-ROOTP = 1
-HEADSQ = 1
-HLAG = 0
-WSCHED = None
+LAST = GROUPS - 1
 
 FLOPS = 2 * GROUPS * P * H * HO
-
-UNITS = [
-    (i * N_TILE, w * N_TILE, c_pass)
-    for (i, w) in [(i, 1) for i in range(DBL)] + [(i, 2) for i in range(DBL, N_BLOCKS, 2)]
-    for c_pass in range(K_PASSES)
-]
 
 
 def interleave(nc, grouped, planes):
@@ -64,18 +45,19 @@ def tile_vocohead_pa_kernel(tc, z1, g1, be1, W2, b2, out):
     nc = tc.nc
     with ExitStack() as ctx:
         const = ctx.enter_context(tc.tile_pool(name="const", bufs=1))
-        inputs = ctx.enter_context(tc.tile_pool(name="inputs", bufs=1))
+        z_pool = ctx.enter_context(tc.tile_pool(name="z_pool", bufs=5))
+        w_pool = ctx.enter_context(tc.tile_pool(name="w_pool", bufs=10))
         keep = ctx.enter_context(tc.tile_pool(name="keep", bufs=1))
         stage = ctx.enter_context(tc.tile_pool(name="stage", bufs=3))
         stats = ctx.enter_context(tc.tile_pool(name="stats", bufs=4))
-        results = ctx.enter_context(tc.tile_pool(name="results", bufs=20))
+        results = ctx.enter_context(tc.tile_pool(name="results", bufs=GROUPS * N_BLOCKS))
         centred_pool = ctx.enter_context(tc.psum_pool(name="centred", bufs=4))
         acc_pool = ctx.enter_context(tc.psum_pool(name="acc", bufs=ACC_BANKS))
 
-        w_codes = keep.tile([P, K_PASSES, HO], U32, align_bytes=64)
-        w_scales = keep.tile([P, K_PASSES, HO], U8, align_bytes=64)
-        h_codes = keep.tile([P, GROUPS, K_PASSES * P], U32, align_bytes=64)
-        h_scales = keep.tile([P, GROUPS, K_PASSES * P], U8, align_bytes=64)
+        w_codes = keep.tile([P, W_OPERANDS, N_TILE], U32, align_bytes=64)
+        w_scales = keep.tile([P, W_OPERANDS, N_TILE], U8, align_bytes=64)
+        h_codes = keep.tile([P, PAIRS, 2 * P], U32, align_bytes=64)
+        h_scales = keep.tile([P, PAIRS, 2 * P], U8, align_bytes=64)
 
         banks = {}
         sumsq = {}
@@ -99,13 +81,12 @@ def tile_vocohead_pa_kernel(tc, z1, g1, be1, W2, b2, out):
                 )
             banks[(pair, j)] = bank
 
-        def squares(pair, j):
-            if j == 0:
-                sumsq[pair] = stats.tile([P, PAIR_CHUNKS], F32, name="sumsq")
-            unread = stage.tile([P, PACK, P], BF16, name="unread")
-            for i in range(j * PACK, (j + 1) * PACK):
+        def squares(pair):
+            sumsq[pair] = stats.tile([P, PAIR_CHUNKS], F32, name="sumsq")
+            unread = stage.tile([P, PAIR_CHUNKS, P], BF16, name="unread")
+            for i in range(PAIR_CHUNKS):
                 nc.scalar.activation(
-                    out=unread[:, i % PACK, :],
+                    out=unread[:, i, :],
                     in_=banks[(pair, i // PACK)][:, i % PACK, :],
                     func=ACT.Square,
                     accum_out=sumsq[pair][:, i : i + 1],
@@ -124,166 +105,120 @@ def tile_vocohead_pa_kernel(tc, z1, g1, be1, W2, b2, out):
         def scale_gain(pair):
             first = (pair % 2) * PAIR_CHUNKS
             gain[pair] = stats.tile([P, PAIR_CHUNKS], F32, name="gain")
-            nc.vector.tensor_mul(
-                out=gain[pair][:], in0=inverse[pair][:], in1=gain0[:, first : first + PAIR_CHUNKS]
+            nc.vector.scalar_tensor_tensor(
+                out=gain[pair][:],
+                in0=inverse[pair][:],
+                scalar=BN_EPS**-0.5,
+                in1=affine[:, 0, first : first + PAIR_CHUNKS],
+                op0=ALU.mult,
+                op1=ALU.mult,
             )
 
-        def whole(b):
-            return b < MERGE_H
-
         def normalise(pair, j):
-            b = pair // 2
             if j == 0:
-                if whole(b):
-                    if pair % 2 == 0:
-                        g_planes = stage.tile([P, PACK, K_PASSES, P], BF16, name="g_planes")
-                        planes[pair] = g_planes
-                        planes[pair + 1] = g_planes
-                else:
-                    p_planes = stage.tile([P, PACK, 2, P], BF16, name="p_planes")
-                    planes[pair] = p_planes
-            slot_in = (2 * (pair % 2) if whole(b) else 0) + j
+                planes[pair] = stage.tile([P, PACK, 2, P], BF16, name="planes")
             for t in range(PACK):
                 i = j * PACK + t
                 a = (pair % 2) * PAIR_CHUNKS + i
                 nc.scalar.activation(
-                    out=planes[pair][:, t, slot_in, :],
+                    out=planes[pair][:, t, j, :],
                     in_=banks[(pair, j)][:, t, :],
                     func=ACT.Relu,
-                    bias=shift[:, a : a + 1],
+                    bias=affine[:, 1, a : a + 1],
                     scale=gain[pair][:, i : i + 1],
                 )
 
         def interleave_h(pair):
-            if whole(pair // 2):
-                grouped = stage.tile([P, K_PASSES * P, PACK], BF16, align_bytes=64, name="g_grouped")
-                s_words = 2 * S_WORDS
-            else:
-                grouped = stage.tile([P, 2 * P, PACK], BF16, align_bytes=64, name="p_grouped")
-                s_words = S_LATE if pair >= LATE_FROM else S_WORDS
-            h_grouped[pair] = grouped
-            words = grouped[:]
+            h_grouped[pair] = stage.tile([P, 2, P, PACK], BF16, align_bytes=64, name="h_grouped")
+            words = h_grouped[pair][:].rearrange("p j r t -> p (j r) t")
             rows = planes[pair][:].rearrange("p t j r -> p t (j r)")
-            if s_words:
-                nc.scalar.copy(
-                    out=words[:, 0:s_words, :].rearrange("p (m i) t -> p m t i", i=RUN),
-                    in_=rows[:, :, 0:s_words].rearrange("p t (m i) -> p m t i", i=RUN),
-                )
-            interleave(nc, words[:, s_words:, :], rows[:, :, s_words:])
+            nc.scalar.copy(
+                out=words[:, 0:S_WORDS, :].rearrange("p (m i) t -> p m t i", i=RUN),
+                in_=rows[:, :, 0:S_WORDS].rearrange("p t (m i) -> p m t i", i=RUN),
+            )
+            interleave(nc, words[:, S_WORDS:, :], rows[:, :, S_WORDS:])
 
         def quantise_h(pair):
-            b = pair // 2
-            cols = slice(0, K_PASSES * P) if whole(b) else slice((pair % 2) * 2 * P, (pair % 2 + 1) * 2 * P)
             nc.vector.quantize_mx(
-                out=h_codes[:, b, cols].bitcast(FP8X4),
-                scales=h_scales[:, b, cols],
-                in_=h_grouped[pair][:].rearrange("p w t -> p (w t)"),
+                out=h_codes[:, pair, :].bitcast(FP8X4),
+                scales=h_scales[:, pair, :],
+                in_=h_grouped[pair][:].rearrange("p j r t -> p (j r t)"),
             )
 
-        def interleave_w(u):
-            first, width, c = UNITS[u]
-            w_grp = stage.tile([P, width, PACK], BF16, align_bytes=64, name="w_grouped%d" % width)
-            w_grouped[u] = w_grp
-            interleave(nc, w_grp[:], w_raw[u][:])
+        def interleave_w(k):
+            w_grouped[k] = stage.tile([P, N_TILE, PACK], BF16, align_bytes=64, name="w_grouped")
+            interleave(nc, w_grouped[k][:], w_raw[k][:])
 
-        def interleave_w_part(u, lo, hi, eng):
-            first, width, c = UNITS[u]
-            if u not in w_grouped:
-                w_grp = stage.tile([P, width, PACK], BF16, align_bytes=64, name="w_grouped%d" % width)
-                w_grouped[u] = w_grp
-            dst = w_grouped[u][:, lo:hi, :].rearrange("p (m i) t -> p m t i", i=RUN)
-            src = w_raw[u][:, :, lo:hi].rearrange("p t (m i) -> p m t i", i=RUN)
-            if eng == "S":
-                nc.scalar.copy(out=dst, in_=src)
-            else:
-                nc.vector.tensor_copy(out=dst, in_=src)
-
-        def quantise_w(u):
-            first, width, c = UNITS[u]
+        def quantise_w(k):
             nc.vector.quantize_mx(
-                out=w_codes[:, c, first : first + width].bitcast(FP8X4),
-                scales=w_scales[:, c, first : first + width],
-                in_=w_grouped[u][:].rearrange("p n t -> p (n t)"),
+                out=w_codes[:, k, :].bitcast(FP8X4),
+                scales=w_scales[:, k, :],
+                in_=w_grouped[k][:].rearrange("p n t -> p (n t)"),
             )
 
         def multiply(b, nb, acc=None, passes=range(K_PASSES)):
             if acc is None:
                 acc = acc_pool.tile([P, N_TILE], F32, name="acc")
-            n0 = nb * N_TILE
             for c in passes:
-                rows = slice(c * P, (c + 1) * P)
+                rows = slice((c % 2) * P, (c % 2 + 1) * P)
                 nc.tensor.matmul_mx(
                     out=acc[:],
-                    lhsT=h_codes[:, b, rows].bitcast(FP8X4),
-                    lhsT_scale=h_scales[:, b, rows],
-                    rhs=w_codes[:, c, n0 : n0 + N_TILE].bitcast(FP8X4),
-                    rhs_scale=w_scales[:, c, n0 : n0 + N_TILE],
+                    lhsT=h_codes[:, 2 * b + c // 2, rows].bitcast(FP8X4),
+                    lhsT_scale=h_scales[:, 2 * b + c // 2, rows],
+                    rhs=w_codes[:, K_PASSES * nb + c, :].bitcast(FP8X4),
+                    rhs_scale=w_scales[:, K_PASSES * nb + c, :],
                     start=(c == 0),
                     stop=(c == K_PASSES - 1),
                 )
             return acc
 
-        def add_bias_and_store(acc, b, nb, pieces=1):
-            n0 = nb * N_TILE
+        def add_bias_and_store(acc, b, nb):
             result = results.tile([P, N_TILE], F32, name="result")
-            w = N_TILE // pieces
-            for i in range(pieces):
-                nc.vector.tensor_tensor(
-                    out=result[:, i * w : (i + 1) * w],
-                    in0=acc[:, i * w : (i + 1) * w],
-                    in1=b2_all[:, n0 + i * w : n0 + (i + 1) * w],
-                    op=ALU.add,
-                )
-                nc.sync.dma_start(out=out[b, :, n0 + i * w : n0 + (i + 1) * w], in_=result[:, i * w : (i + 1) * w])
+            width = N_TILE // 2 if (b, nb) == (LAST, N_BLOCKS - 1) else N_TILE
+            for first in range(0, N_TILE, width):
+                part = slice(first, first + width)
+                cols = slice(nb * N_TILE + first, nb * N_TILE + first + width)
+                nc.vector.tensor_tensor(out=result[:, part], in0=acc[:, part], in1=b2_all[:, cols], op=ALU.add)
+                nc.sync.dma_start(out=out[b, :, cols], in_=result[:, part])
 
         with tc.manual_schedule():
             pass_rows = const.tile([P, PACK * P], BF16)
+            nc.vector.memset(pass_rows[:].bitcast(U32), 0)
             b2_all = const.tile([P, HO], BF16)
             z_sb = []
             w_raw = []
 
-            def load_weights(u):
-                first, width, c = UNITS[u]
-                w_tile = inputs.tile([P, PACK, width], BF16, name="w%d" % u)
+            def load_weights(k):
+                nb, c = divmod(k, K_PASSES)
+                w_tile = w_pool.tile([P, PACK, N_TILE], BF16, name="w_tile")
                 nc.sync.dma_start(
                     out=w_tile[:],
                     in_=W2[
-                        c * PACK * P : (c + 1) * PACK * P, first : first + width
+                        c * PACK * P : (c + 1) * PACK * P, nb * N_TILE : (nb + 1) * N_TILE
                     ].rearrange("(p t) n -> p t n", t=PACK),
                 )
                 w_raw.append(w_tile)
 
             def load_group(b, first, last):
+                if first == 0:
+                    z_tile = z_pool.tile([P, H], BF16, name="z_tile")
+                    z_sb.append(z_tile)
                 cols = slice(first * PACK * P, last * PACK * P)
                 nc.sync.dma_start(out=z_sb[b][:, cols], in_=z1[b, :, cols])
 
-            for b in range(GROUPS):
-                z_tile = inputs.tile([P, H], BF16, name="z%d" % b)
-                z_sb.append(z_tile)
             load_weights(0)
             load_group(0, 0, 2)
             load_weights(1)
-            nc.vector.memset(pass_rows[:].bitcast(U32), 0)
             for i, vector in enumerate((g1, be1, b2)):
                 nc.sync.dma_start(
                     out=pass_rows[i * K_PASSES : (i + 1) * K_PASSES, :],
                     in_=vector.rearrange("(c f) -> c f", c=K_PASSES),
                 )
             load_group(0, 2, 4)
-            loaded = 2
-            total_cols = 0
             for b in range(1, GROUPS):
-                want = b * 2 * N_TILE + N_TILE
-                while loaded < len(UNITS) and sum(UNITS[x][1] for x in range(loaded)) < want:
-                    load_weights(loaded)
-                    loaded += 1
+                load_weights(2 * b)
                 load_group(b, 0, 4)
-                while loaded < len(UNITS) and sum(UNITS[x][1] for x in range(loaded)) < want + N_TILE:
-                    load_weights(loaded)
-                    loaded += 1
-            while loaded < len(UNITS):
-                load_weights(loaded)
-                loaded += 1
+                load_weights(2 * b + 1)
 
             ident = const.tile([P, P], BF16)
             make_identity(nc, ident[:])
@@ -295,178 +230,97 @@ def tile_vocohead_pa_kernel(tc, z1, g1, be1, W2, b2, out):
             nc.scalar.activation(out=warm[:], in_=one[:], func=ACT.Abs_reciprocal_sqrt)
 
             def spread_b2(half):
-                src = b2_banks[half][:].rearrange("p a n -> p (a n)")
-                dst = b2_all[:, half * 2 * N_TILE : (half + 1) * 2 * N_TILE]
-                if B2S:
-                    nc.scalar.copy(out=dst, in_=src)
-                else:
-                    nc.vector.tensor_copy(out=dst, in_=src)
+                nc.vector.tensor_copy(
+                    out=b2_all[:, half * 2 * N_TILE : (half + 1) * 2 * N_TILE],
+                    in_=b2_banks[half][:].rearrange("p a n -> p (a n)"),
+                )
 
-            interleave_w_part(0, 0, 512, "V")
+            interleave_w(0)
             centre(0, 0)
             centre(0, 1)
-            squares(0, 0)
-            squares(0, 1)
+            squares(0)
             root(0)
             quantise_w(0)
-            interleave_w_part(1, 0, 512, "V")
-            features_ps = acc_pool.tile([P, 2 * PACK, P], BF16, name="acc")
+            interleave_w(1)
+            features_ps = acc_pool.tile([P, PACK, P], BF16, name="acc")
             for t in range(PACK):
                 nc.tensor.transpose(
                     out=features_ps[:, t, :], in_=pass_rows[:, t : PACK * P : PACK], identity=ident[:]
                 )
-            for s in range(PACK):
-                nc.tensor.transpose(
-                    out=features_ps[:, PACK + s, :], in_=pass_rows[:, s * P : (s + 1) * P], identity=ident[:]
-                )
             centre(1, 0)
             centre(1, 1)
-            if HEADSQ:
-                squares(1, 0)
-                squares(1, 1)
-                root(1)
-            gain0 = const.tile([P, CHUNKS], F32)
-            nc.vector.tensor_scalar_mul(
-                out=gain0[:].rearrange("p (c t) -> p t c", t=PACK),
-                in0=features_ps[:, 0:PACK, 0:K_PASSES],
-                scalar1=BN_EPS**-0.5,
-            )
-            shift = const.tile([P, CHUNKS], F32)
+            squares(1)
+            root(1)
+            affine = const.tile([P, 2, CHUNKS], F32)
             nc.vector.tensor_copy(
-                out=shift[:].rearrange("p (c t) -> p t c", t=PACK),
-                in_=features_ps[:, 0:PACK, K_PASSES : 2 * K_PASSES],
+                out=affine[:].rearrange("p v (c t) -> p t (v c)", t=PACK),
+                in_=features_ps[:, :, 0 : 2 * K_PASSES],
             )
             scale_gain(0)
-            b2_columns = const.tile([P, PACK, K_PASSES], BF16)
-            nc.vector.tensor_copy(
-                out=b2_columns[:], in_=features_ps[:, PACK : 2 * PACK, 2 * K_PASSES : 3 * K_PASSES]
-            )
             b2_banks = []
             for half in range(2):
-                b2_ps = acc_pool.tile([P, 2 * PACK, P], BF16, name="acc")
-                for i in range(2 * PACK):
-                    c, s = divmod(2 * PACK * half + i, PACK)
+                b2_ps = acc_pool.tile([P, 2, N_TILE], BF16, name="acc")
+                for i in range(2):
+                    row = 2 * K_PASSES + 2 * half + i
                     nc.tensor.matmul(
                         out=b2_ps[:, i, :],
-                        lhsT=b2_columns[:, s, c : c + 1].to_broadcast([P, P]),
-                        rhs=ident[:],
+                        lhsT=ident[:, row : row + 1].to_broadcast([P, P]),
+                        rhs=pass_rows[:],
                         start=True,
                         stop=True,
                     )
                 b2_banks.append(b2_ps)
             quantise_w(1)
             interleave_w(2)
-            if HEADSQ:
-                scale_gain(1)
-            if not B2S:
-                spread_b2(0)
+            scale_gain(1)
+            spread_b2(0)
             quantise_w(2)
-            if HEADW > 3:
-                interleave_w(3)
-            if not B2S:
-                spread_b2(1)
-            if HEADW > 3:
-                quantise_w(3)
+            interleave_w(3)
+            spread_b2(1)
+            quantise_w(3)
 
-        LAST = GROUPS - 1
         last_acc = []
-        half_acc = {}
         multiplied = set()
         in_psum = []
         slot = 0
-        w_done = HEADW
-        ready_cols = 0
-        sched = WSCHED if WSCHED is not None else [1] * 40
         while len(multiplied) < GROUPS * N_BLOCKS or in_psum:
-            nxt = slot + 1 if (1 - HEADSQ) <= slot + 0 and slot + 1 < PAIRS and not (HEADSQ and slot == 0) else None
-            if slot < PAIRS:
-                if nxt is not None:
-                    squares(nxt, 0)
-                    if SMODE == 0:
-                        squares(nxt, 1)
-                        if ROOTP == 0:
-                            root(nxt)
-                normalise(slot, 0)
+            next_pair = slot + 1 if 1 <= slot < PAIRS - 1 else None
+            if next_pair is not None:
+                squares(next_pair)
+            for j in range(2):
+                if slot < PAIRS:
+                    normalise(slot, j)
                 if slot + 2 < PAIRS:
-                    centre(slot + 2, 0)
-                if nxt is not None and SMODE == 0 and ROOTP == 1:
-                    root(nxt)
-                if nxt is not None and SMODE == 2:
-                    squares(nxt, 1)
-                    root(nxt)
-                normalise(slot, 1)
-                if slot + 2 < PAIRS:
-                    centre(slot + 2, 1)
-                if nxt is not None and SMODE == 1:
-                    squares(nxt, 1)
-                    root(nxt)
-            due = []
-            if 0 <= slot - HLAG < PAIRS:
-                pair = slot - HLAG
-                if not whole(pair // 2) or pair % 2 == 1:
-                    due = [pair]
-            units = []
-            n_units = sched[slot] if slot < len(sched) else 1
-            while n_units > 0 and w_done < len(UNITS):
-                units.append(w_done)
-                w_done += 1
-                n_units -= 1
-            def run_v(ch):
-                if ch == "A":
-                    for pair in due:
-                        interleave_h(pair)
-                elif ch == "B":
-                    for u in units:
-                        interleave_w(u)
-                elif ch == "C":
-                    for pair in due:
-                        quantise_h(pair)
-                elif ch == "D":
-                    for acc, b, nb in in_psum[: (len(in_psum) + 1) // 2]:
-                        add_bias_and_store(acc, b, nb)
-                elif ch == "d":
-                    for acc, b, nb in in_psum[(len(in_psum) + 1) // 2 :]:
-                        add_bias_and_store(acc, b, nb)
-                elif ch == "E":
-                    for u in units:
-                        quantise_w(u)
-                elif ch == "F":
-                    if nxt is not None:
-                        scale_gain(nxt)
-            if PINV:
-                with tc.manual_schedule(engines={mybir.EngineType.DVE}):
-                    for ch in ORDER:
-                        run_v(ch)
-            else:
-                for ch in ORDER:
-                    run_v(ch)
-            in_psum = []
+                    centre(slot + 2, j)
+                if j == 1 and next_pair is not None:
+                    root(next_pair)
 
-            pairs_done = slot + 1 - HLAG
-            groups_ready = min(pairs_done // 2, LAST)
-            cols_ready = [sum(1 for x in range(w_done) if UNITS[x][0] <= nb * N_TILE < UNITS[x][0] + UNITS[x][1]) == K_PASSES for nb in range(N_BLOCKS)]
-            cells = [(b, nb) for b in range(groups_ready) for nb in range(N_BLOCKS)]
-            if MXORD == 1:
-                cells.sort(key=lambda x: (x[1], x[0]))
-            if MXORD == 2:
-                cells.sort(key=lambda x: (-x[0], x[1]))
-            for b, nb in cells:
-                if True:
-                    if cols_ready[nb] and (b, nb) not in multiplied and len(in_psum) < ACC_BANKS:
+            k = slot + W_AHEAD
+            if next_pair is not None:
+                scale_gain(next_pair)
+            for tile_in_psum in in_psum:
+                add_bias_and_store(*tile_in_psum)
+            in_psum = []
+            if k < W_OPERANDS:
+                interleave_w(k)
+                quantise_w(k)
+            if slot < PAIRS:
+                interleave_h(slot)
+                quantise_h(slot)
+
+            groups_ready = min((slot + 1) // 2, LAST)
+            blocks_ready = min(k + 1, W_OPERANDS) // K_PASSES
+            for b in range(groups_ready):
+                for nb in range(blocks_ready):
+                    if (b, nb) not in multiplied and len(in_psum) < ACC_BANKS:
                         multiplied.add((b, nb))
                         in_psum.append((multiply(b, nb), b, nb))
-            if pairs_done == PAIRS - 1:
-                if not in_psum and len(multiplied) == LAST * N_BLOCKS:
-                    last_acc = [multiply(LAST, nb, None, (0, 1)) for nb in range(N_BLOCKS)]
-            if pairs_done >= PAIRS:
-                if last_acc:
-                    for nb in range(N_BLOCKS):
-                        if (LAST, nb) not in multiplied:
-                            multiplied.add((LAST, nb))
-                            in_psum.append((multiply(LAST, nb, last_acc[nb], (2, 3)), LAST, nb))
-                else:
-                    for nb in range(N_BLOCKS):
-                        if (LAST, nb) not in multiplied and len(in_psum) < ACC_BANKS:
-                            multiplied.add((LAST, nb))
-                            in_psum.append((multiply(LAST, nb), LAST, nb))
+            if slot == PAIRS - 2:
+                assert len(multiplied) == LAST * N_BLOCKS
+                last_acc = [multiply(LAST, nb, None, (0, 1)) for nb in range(N_BLOCKS - len(in_psum))]
+            if slot == PAIRS - 1:
+                for nb in range(N_BLOCKS):
+                    multiplied.add((LAST, nb))
+                    acc = multiply(LAST, nb, last_acc[nb], (2, 3)) if nb < len(last_acc) else multiply(LAST, nb)
+                    in_psum.append((acc, LAST, nb))
             slot += 1

from contextlib import ExitStack

import concourse.mybir as mybir
from concourse.masks import make_identity

FP8X4 = mybir.dt.float8_e4m3fn_x4
BF16 = mybir.dt.bfloat16
F32 = mybir.dt.float32
U32 = mybir.dt.uint32
U8 = mybir.dt.uint8
ACT = mybir.ActivationFunctionType
ALU = mybir.AluOpType

P = 128
PACK = 4
GROUPS = 8
H = 2048
HO = 2048
K_PASSES = H // (P * PACK)
CHUNKS = H // P
N_TILE = 512
N_BLOCKS = HO // N_TILE
BN_EPS = 1e-5

PAIRS = 2 * GROUPS
PAIR_CHUNKS = 2 * PACK
W_OPERANDS = N_BLOCKS * K_PASSES
W_AHEAD = 4
ACC_BANKS = 4
RUN = 8
S_WORDS = 128
LAST = GROUPS - 1

FLOPS = 2 * GROUPS * P * H * HO


def interleave(nc, grouped, planes):
    nc.vector.tensor_copy(
        out=grouped.rearrange("p (m i) t -> p m t i", i=RUN),
        in_=planes.rearrange("p t (m i) -> p m t i", i=RUN),
    )


def tile_vocohead_pa_kernel(tc, z1, g1, be1, W2, b2, out):
    nc = tc.nc
    with ExitStack() as ctx:
        const = ctx.enter_context(tc.tile_pool(name="const", bufs=1))
        z_pool = ctx.enter_context(tc.tile_pool(name="z_pool", bufs=5))
        w_pool = ctx.enter_context(tc.tile_pool(name="w_pool", bufs=10))
        keep = ctx.enter_context(tc.tile_pool(name="keep", bufs=1))
        stage = ctx.enter_context(tc.tile_pool(name="stage", bufs=3))
        stats = ctx.enter_context(tc.tile_pool(name="stats", bufs=4))
        results = ctx.enter_context(tc.tile_pool(name="results", bufs=GROUPS * N_BLOCKS))
        centred_pool = ctx.enter_context(tc.psum_pool(name="centred", bufs=4))
        acc_pool = ctx.enter_context(tc.psum_pool(name="acc", bufs=ACC_BANKS))

        w_codes = keep.tile([P, W_OPERANDS, N_TILE], U32, align_bytes=64)
        w_scales = keep.tile([P, W_OPERANDS, N_TILE], U8, align_bytes=64)
        h_codes = keep.tile([P, PAIRS, 2 * P], U32, align_bytes=64)
        h_scales = keep.tile([P, PAIRS, 2 * P], U8, align_bytes=64)

        banks = {}
        sumsq = {}
        inverse = {}
        gain = {}
        planes = {}
        h_grouped = {}
        w_grouped = {}

        def centre(pair, j):
            b, first = pair // 2, (pair % 2) * PAIR_CHUNKS + j * PACK
            bank = centred_pool.tile([P, PACK, P], F32, tag="centred")
            for t in range(PACK):
                a = first + t
                nc.tensor.matmul(
                    out=bank[:, t, :],
                    lhsT=z_sb[b][:, (a // PACK) * PACK * P + a % PACK : (a // PACK + 1) * PACK * P : PACK],
                    rhs=centre_matrix[:],
                    start=True,
                    stop=True,
                )
            banks[(pair, j)] = bank

        def squares(pair):
            sumsq[pair] = stats.tile([P, PAIR_CHUNKS], F32, name="sumsq")
            unread = stage.tile([P, PAIR_CHUNKS, P], BF16, name="unread")
            for i in range(PAIR_CHUNKS):
                nc.scalar.activation(
                    out=unread[:, i, :],
                    in_=banks[(pair, i // PACK)][:, i % PACK, :],
                    func=ACT.Square,
                    accum_out=sumsq[pair][:, i : i + 1],
                )

        def root(pair):
            inverse[pair] = stats.tile([P, PAIR_CHUNKS], F32, name="inverse")
            nc.scalar.activation(
                out=inverse[pair][:],
                in_=sumsq[pair][:],
                func=ACT.Abs_reciprocal_sqrt,
                bias=one[:, 0:1],
                scale=1.0 / (P * BN_EPS),
            )

        def scale_gain(pair):
            first = (pair % 2) * PAIR_CHUNKS
            gain[pair] = stats.tile([P, PAIR_CHUNKS], F32, name="gain")
            nc.vector.scalar_tensor_tensor(
                out=gain[pair][:],
                in0=inverse[pair][:],
                scalar=BN_EPS**-0.5,
                in1=affine[:, 0, first : first + PAIR_CHUNKS],
                op0=ALU.mult,
                op1=ALU.mult,
            )

        def normalise(pair, j):
            if j == 0:
                planes[pair] = stage.tile([P, PACK, 2, P], BF16, name="planes")
            for t in range(PACK):
                i = j * PACK + t
                a = (pair % 2) * PAIR_CHUNKS + i
                nc.scalar.activation(
                    out=planes[pair][:, t, j, :],
                    in_=banks[(pair, j)][:, t, :],
                    func=ACT.Relu,
                    bias=affine[:, 1, a : a + 1],
                    scale=gain[pair][:, i : i + 1],
                )

        def interleave_h(pair):
            h_grouped[pair] = stage.tile([P, 2, P, PACK], BF16, align_bytes=64, name="h_grouped")
            words = h_grouped[pair][:].rearrange("p j r t -> p (j r) t")
            rows = planes[pair][:].rearrange("p t j r -> p t (j r)")
            nc.scalar.copy(
                out=words[:, 0:S_WORDS, :].rearrange("p (m i) t -> p m t i", i=RUN),
                in_=rows[:, :, 0:S_WORDS].rearrange("p t (m i) -> p m t i", i=RUN),
            )
            interleave(nc, words[:, S_WORDS:, :], rows[:, :, S_WORDS:])

        def quantise_h(pair):
            nc.vector.quantize_mx(
                out=h_codes[:, pair, :].bitcast(FP8X4),
                scales=h_scales[:, pair, :],
                in_=h_grouped[pair][:].rearrange("p j r t -> p (j r t)"),
            )

        def interleave_w(k):
            w_grouped[k] = stage.tile([P, N_TILE, PACK], BF16, align_bytes=64, name="w_grouped")
            interleave(nc, w_grouped[k][:], w_raw[k][:])

        def quantise_w(k):
            nc.vector.quantize_mx(
                out=w_codes[:, k, :].bitcast(FP8X4),
                scales=w_scales[:, k, :],
                in_=w_grouped[k][:].rearrange("p n t -> p (n t)"),
            )

        def multiply(b, nb, acc=None, passes=range(K_PASSES)):
            if acc is None:
                acc = acc_pool.tile([P, N_TILE], F32, name="acc")
            for c in passes:
                rows = slice((c % 2) * P, (c % 2 + 1) * P)
                nc.tensor.matmul_mx(
                    out=acc[:],
                    lhsT=h_codes[:, 2 * b + c // 2, rows].bitcast(FP8X4),
                    lhsT_scale=h_scales[:, 2 * b + c // 2, rows],
                    rhs=w_codes[:, K_PASSES * nb + c, :].bitcast(FP8X4),
                    rhs_scale=w_scales[:, K_PASSES * nb + c, :],
                    start=(c == 0),
                    stop=(c == K_PASSES - 1),
                )
            return acc

        def add_bias_and_store(acc, b, nb):
            result = results.tile([P, N_TILE], F32, name="result")
            width = N_TILE // 2 if (b, nb) == (LAST, N_BLOCKS - 1) else N_TILE
            for first in range(0, N_TILE, width):
                part = slice(first, first + width)
                cols = slice(nb * N_TILE + first, nb * N_TILE + first + width)
                nc.vector.tensor_tensor(out=result[:, part], in0=acc[:, part], in1=b2_all[:, cols], op=ALU.add)
                nc.sync.dma_start(out=out[b, :, cols], in_=result[:, part])

        with tc.manual_schedule():
            pass_rows = const.tile([P, PACK * P], BF16)
            nc.vector.memset(pass_rows[:].bitcast(U32), 0)
            b2_all = const.tile([P, HO], BF16)
            z_sb = []
            w_raw = []

            def load_weights(k):
                nb, c = divmod(k, K_PASSES)
                w_tile = w_pool.tile([P, PACK, N_TILE], BF16, name="w_tile")
                nc.sync.dma_start(
                    out=w_tile[:],
                    in_=W2[
                        c * PACK * P : (c + 1) * PACK * P, nb * N_TILE : (nb + 1) * N_TILE
                    ].rearrange("(p t) n -> p t n", t=PACK),
                )
                w_raw.append(w_tile)

            def load_group(b, first, last):
                if first == 0:
                    z_tile = z_pool.tile([P, H], BF16, name="z_tile")
                    z_sb.append(z_tile)
                cols = slice(first * PACK * P, last * PACK * P)
                nc.sync.dma_start(out=z_sb[b][:, cols], in_=z1[b, :, cols])

            load_weights(0)
            load_group(0, 0, 2)
            load_weights(1)
            for i, vector in enumerate((g1, be1, b2)):
                nc.sync.dma_start(
                    out=pass_rows[i * K_PASSES : (i + 1) * K_PASSES, :],
                    in_=vector.rearrange("(c f) -> c f", c=K_PASSES),
                )
            load_group(0, 2, 4)
            for b in range(1, GROUPS):
                load_weights(2 * b)
                load_group(b, 0, 4)
                load_weights(2 * b + 1)

            ident = const.tile([P, P], BF16)
            make_identity(nc, ident[:])
            centre_matrix = const.tile([P, P], BF16)
            nc.vector.tensor_scalar_add(out=centre_matrix[:], in0=ident[:], scalar1=-1.0 / P)
            one = const.tile([P, 1], F32)
            nc.vector.memset(one[:], 1.0)
            warm = const.tile([P, 1], F32)
            nc.scalar.activation(out=warm[:], in_=one[:], func=ACT.Abs_reciprocal_sqrt)

            def spread_b2(half):
                nc.vector.tensor_copy(
                    out=b2_all[:, half * 2 * N_TILE : (half + 1) * 2 * N_TILE],
                    in_=b2_banks[half][:].rearrange("p a n -> p (a n)"),
                )

            interleave_w(0)
            centre(0, 0)
            centre(0, 1)
            squares(0)
            root(0)
            quantise_w(0)
            interleave_w(1)
            features_ps = acc_pool.tile([P, PACK, P], BF16, name="acc")
            for t in range(PACK):
                nc.tensor.transpose(
                    out=features_ps[:, t, :], in_=pass_rows[:, t : PACK * P : PACK], identity=ident[:]
                )
            centre(1, 0)
            centre(1, 1)
            squares(1)
            root(1)
            affine = const.tile([P, 2, CHUNKS], F32)
            nc.vector.tensor_copy(
                out=affine[:].rearrange("p v (c t) -> p t (v c)", t=PACK),
                in_=features_ps[:, :, 0 : 2 * K_PASSES],
            )
            scale_gain(0)
            b2_banks = []
            for half in range(2):
                b2_ps = acc_pool.tile([P, 2, N_TILE], BF16, name="acc")
                for i in range(2):
                    row = 2 * K_PASSES + 2 * half + i
                    nc.tensor.matmul(
                        out=b2_ps[:, i, :],
                        lhsT=ident[:, row : row + 1].to_broadcast([P, P]),
                        rhs=pass_rows[:],
                        start=True,
                        stop=True,
                    )
                b2_banks.append(b2_ps)
            quantise_w(1)
            interleave_w(2)
            scale_gain(1)
            spread_b2(0)
            quantise_w(2)
            interleave_w(3)
            spread_b2(1)
            quantise_w(3)

        last_acc = []
        multiplied = set()
        in_psum = []
        slot = 0
        while len(multiplied) < GROUPS * N_BLOCKS or in_psum:
            next_pair = slot + 1 if 1 <= slot < PAIRS - 1 else None
            if next_pair is not None:
                squares(next_pair)
            for j in range(2):
                if slot < PAIRS:
                    normalise(slot, j)
                if slot + 2 < PAIRS:
                    centre(slot + 2, j)
                if j == 1 and next_pair is not None:
                    root(next_pair)

            k = slot + W_AHEAD
            if next_pair is not None:
                scale_gain(next_pair)
            for tile_in_psum in in_psum:
                add_bias_and_store(*tile_in_psum)
            in_psum = []
            if k < W_OPERANDS:
                interleave_w(k)
                quantise_w(k)
            if slot < PAIRS:
                interleave_h(slot)
                quantise_h(slot)

            groups_ready = min((slot + 1) // 2, LAST)
            blocks_ready = min(k + 1, W_OPERANDS) // K_PASSES
            for b in range(groups_ready):
                for nb in range(blocks_ready):
                    if (b, nb) not in multiplied and len(in_psum) < ACC_BANKS:
                        multiplied.add((b, nb))
                        in_psum.append((multiply(b, nb), b, nb))
            if slot == PAIRS - 2:
                assert len(multiplied) == LAST * N_BLOCKS
                last_acc = [multiply(LAST, nb, None, (0, 1)) for nb in range(N_BLOCKS - len(in_psum))]
            if slot == PAIRS - 1:
                for nb in range(N_BLOCKS):
                    multiplied.add((LAST, nb))
                    acc = multiply(LAST, nb, last_acc[nb], (2, 3)) if nb < len(last_acc) else multiply(LAST, nb)
                    in_psum.append((acc, LAST, nb))
            slot += 1
